import numpy as np
import ml_dtypes


def mxq(x, axis, fmt="e4m3"):
    dtype, down = {"e4m3": (ml_dtypes.float8_e4m3fn, 7), "e5m2": (ml_dtypes.float8_e5m2, 14)}[fmt]
    v = np.moveaxis(np.asarray(x, np.float32).astype(ml_dtypes.bfloat16).astype(np.float64), axis, -1)
    blocks = v.reshape(v.shape[:-1] + (-1, 32))
    amax = np.abs(blocks).max(-1, keepdims=True)
    byte = np.maximum(np.where(amax > 0, np.frexp(amax)[1] - 1 + 127, 0) - down, 1)
    scale = np.exp2(byte - 127.0)
    codes = (blocks / scale).astype(np.float32).astype(dtype).astype(np.float64)
    return np.moveaxis((codes * scale).reshape(v.shape), -1, axis)


WIDE = False


def mx_kscale(k):
    if not WIDE:
        return np.ones(k)
    levels = np.array([10, -10, 5, -5, 0])
    a = np.random.permutation(np.resize(levels, k // 512 * 4)).reshape(k // 512, 4)
    idx = np.arange(k)
    return np.exp2(a[idx // 512, idx % 128 // 32])


BF16 = ml_dtypes.bfloat16


def bf(x):
    return np.asarray(x, np.float32).astype(BF16)


def f64(x):
    return np.asarray(x).astype(np.float64)


E2M1 = np.array([0.0, 0.5, 1.0, 1.5, 2.0, 3.0, 4.0, 6.0, -0.0, -0.5, -1.0, -1.5, -2.0, -3.0, -4.0, -6.0])


def pack_weight(w, fmt):
    k, n = w.shape
    w = f64(bf(w)).reshape(k // 32, 32, n)
    amax = np.abs(w).max(1)
    if fmt == "e4m3":
        byte = np.frexp(amax)[1] - 1 + 127 - 7
    else:
        mant, ex = np.frexp(amax / 6.0)
        byte = np.where(mant > 0.5, ex, ex - 1) + 127
    byte = np.clip(np.where(amax > 0, byte, 1), 1, 254)
    scaled = (w * np.exp2(127.0 - byte)[:, None, :]).reshape(k, n).astype(np.float32)
    by_word = np.ascontiguousarray(scaled.reshape(k // 512, 128, 4, n).transpose(0, 1, 3, 2))
    if fmt == "e4m3":
        words = by_word.astype(ml_dtypes.float8_e4m3fn).view(np.uint8)
    else:
        c = by_word.astype(ml_dtypes.float4_e2m1fn).view(np.uint8) & 0xF
        words = c[..., 0::2] | (c[..., 1::2] << 4)
    return np.ascontiguousarray(words), np.ascontiguousarray(byte.astype(np.uint8).reshape(k // 512, 16, n))


def unpack_weight(words, scales, fmt):
    g, p, n, _ = words.shape
    if fmt == "e4m3":
        vals = np.ascontiguousarray(words).view(ml_dtypes.float8_e4m3fn).astype(np.float64)
    else:
        nib = np.empty((g, p, n, 4), np.uint8)
        nib[..., 0::2] = words & 0xF
        nib[..., 1::2] = words >> 4
        vals = E2M1[nib]
    vals = vals * np.repeat(np.exp2(scales.astype(np.float64) - 127.0), 8, axis=1)[..., None]
    return vals.transpose(0, 1, 3, 2).reshape(g * 512, n)


S, DIM, NH, NKV, HD, HID = 512, 16384, 8, 4, 32, 4096
EPS = 1e-6
ROPE_THETA = 10000.0
FMT = "e4m3"


def rmsnorm(x, w):
    return x * (1.0 / np.sqrt(np.mean(x * x, axis=-1, keepdims=True) + EPS)) * w


def rope(t, cos, sin):
    te, to = t[..., 0::2], t[..., 1::2]
    c, s = cos[:, None, :], sin[:, None, :]
    re = te * c - to * s
    ro = te * s + to * c
    return np.stack([re, ro], axis=-1).reshape(t.shape)


def setup_inputs():
    s = mx_kscale(DIM)
    inv_freq = 1.0 / (ROPE_THETA ** (np.arange(0, HD, 2) / HD))
    ang = np.outer(np.arange(S), inv_freq)
    a = 1.0 / np.sqrt(DIM)
    x = bf(np.random.standard_normal((S, DIM)))
    freqs_cos = bf(np.cos(ang))
    freqs_sin = bf(np.sin(ang))
    wq_words, wq_scales = pack_weight((np.random.standard_normal((NH * HD, DIM)) * 1.5 * a / s).T, FMT)
    wk_words, wk_scales = pack_weight((np.random.standard_normal((NKV * HD, DIM)) * 1.5 * a / s).T, FMT)
    wv_words, wv_scales = pack_weight((np.random.standard_normal((NKV * HD, DIM)) * a / s).T, FMT)
    attn_norm_w = bf((1.0 + 0.1 * np.random.standard_normal(DIM)) * s)
    return {"x": x,
            "freqs_cos": freqs_cos,
            "freqs_sin": freqs_sin,
            "wq_words": wq_words,
            "wq_scales": wq_scales,
            "wk_words": wk_words,
            "wk_scales": wk_scales,
            "wv_words": wv_words,
            "wv_scales": wv_scales,
            "attn_norm_w": attn_norm_w}


def reference(x, freqs_cos, freqs_sin, wq_words, wq_scales, wk_words, wk_scales, wv_words, wv_scales, attn_norm_w):
    hq = mxq(rmsnorm(f64(x), f64(attn_norm_w)), 1, "e4m3")
    q = (hq @ unpack_weight(wq_words, wq_scales, FMT)).reshape(S, NH, HD)
    k = (hq @ unpack_weight(wk_words, wk_scales, FMT)).reshape(S, NKV, HD)
    v = (hq @ unpack_weight(wv_words, wv_scales, FMT)).reshape(S, NKV, HD)
    c, sn = f64(freqs_cos), f64(freqs_sin)
    return rope(q, c, sn), rope(k, c, sn), v

@@ -1,0 +1,290 @@
+from contextlib import ExitStack
+
+import concourse.mybir as mybir
+from concourse.masks import make_identity
+
+F32 = mybir.dt.float32
+BF16 = mybir.dt.bfloat16
+I32 = mybir.dt.int32
+U32 = mybir.dt.uint32
+U8 = mybir.dt.uint8
+FP8X4 = mybir.dt.float8_e4m3fn_x4
+ACT = mybir.ActivationFunctionType
+ALU = mybir.AluOpType
+AXIS = mybir.AxisListType
+
+P = 128
+TOKENS = 512
+DIM = 16384
+EPS = 1e-6
+TOKEN_TILES = TOKENS // P
+K_PASS = 4 * P
+PASSES = DIM // K_PASS
+RUN = 4
+RUN_K = RUN * K_PASS
+RUNS = PASSES // RUN
+N_Q, N_K, N_V = 256, 128, 128
+N_OUT = N_Q + N_K + N_V
+N_ROPE = N_Q + N_K
+HEADS = N_ROPE // 32
+PAIRS = 16
+W_BLOCK = 8
+
+FLOPS = 2 * TOKENS * DIM * N_OUT
+
+
+def tile_transformerblock_pa_k_kernel(
+    tc,
+    x,
+    freqs_cos,
+    freqs_sin,
+    wq_words,
+    wq_scales,
+    wk_words,
+    wk_scales,
+    wv_words,
+    wv_scales,
+    attn_norm_w,
+    out_0,
+    out_1,
+    out_2,
+):
+    nc = tc.nc
+    weights = ((wq_words, wq_scales, 0, N_Q), (wk_words, wk_scales, N_Q, N_K), (wv_words, wv_scales, N_ROPE, N_V))
+
+    with ExitStack() as stack:
+        keep = stack.enter_context(tc.tile_pool(name="keep", bufs=1))
+        x_pool = stack.enter_context(tc.tile_pool(name="x_pool", bufs=2 * RUNS))
+        h_pool = stack.enter_context(tc.tile_pool(name="h_pool", bufs=2))
+        grouped_pool = stack.enter_context(tc.tile_pool(name="grouped_pool", bufs=2))
+        code_pool = stack.enter_context(tc.tile_pool(name="code_pool", bufs=6))
+        scrap_pool = stack.enter_context(tc.tile_pool(name="scrap_pool", bufs=1))
+        small_pool = stack.enter_context(tc.tile_pool(name="small_pool", bufs=2))
+        out_pool = stack.enter_context(tc.tile_pool(name="out_pool", bufs=2))
+        rope_pool = stack.enter_context(tc.tile_pool(name="rope_pool", bufs=1))
+        bank_pool = stack.enter_context(tc.psum_pool(name="bank_pool", bufs=6))
+        acc_pool = stack.enter_context(tc.psum_pool(name="acc_pool", bufs=2))
+
+        eps_col = keep.tile([P, 1], F32)
+        nc.vector.memset(eps_col[:], EPS)
+        warm = keep.tile([P, 1], F32)
+        nc.scalar.activation(out=warm[:], in_=eps_col[:], func=ACT.Sqrt)
+
+        ident_f32 = keep.tile([P, P], F32)
+        make_identity(nc, ident_f32[:])
+        ident_bf16 = keep.tile([P, P], BF16)
+        make_identity(nc, ident_bf16[:])
+
+        sums = keep.tile([P, TOKEN_TILES, 16], F32)
+        nc.vector.memset(sums[:], 0.0)
+        rstd = keep.tile([P, TOKEN_TILES], F32)
+
+        w_words = keep.tile([P, PASSES, N_OUT], I32, align_bytes=64)
+        w_planes = keep.tile([P, PASSES, N_OUT], U8, align_bytes=64)
+        nc.vector.memset(w_planes[:].rearrange("p g n -> p (g n)").bitcast(I32), 0)
+        for quadrant in range(4):
+            for unused_words, scales, first, width in weights:
+                nc.gpsimd.dma_start(
+                    out=w_planes[32 * quadrant : 32 * quadrant + 4, :, first : first + width].bitcast(F32),
+                    in_=scales[:, 4 * quadrant : 4 * quadrant + 4, :].rearrange("g q n -> q g n").bitcast(F32),
+                )
+
+        gain_rows = keep.tile([P, K_PASS], BF16)
+        nc.vector.memset(gain_rows[:], 0.0)
+        nc.sync.dma_start(out=gain_rows[0:PASSES, :], in_=attn_norm_w.rearrange("(c n) -> c n", n=K_PASS))
+
+        x_pieces = {}
+
+        def load_x(m, r):
+            piece = x_pool.tile([P, RUN_K], BF16)
+            nc.sync.dma_start(out=piece[:], in_=x[P * m : P * (m + 1), RUN_K * r : RUN_K * (r + 1)])
+            x_pieces[(m, r)] = piece
+
+        for m in range(2):
+            for r in range(RUNS):
+                load_x(m, r)
+
+        for block in range(PASSES // W_BLOCK):
+            passes = slice(W_BLOCK * block, W_BLOCK * (block + 1))
+            for words, unused_scales, first, width in weights:
+                nc.sync.dma_start(
+                    out=w_words[:, passes, first : first + width],
+                    in_=words[passes].rearrange("g p n t -> p g (n t)").bitcast(I32),
+                )
+
+        cos_bf16 = keep.tile([P, TOKEN_TILES, PAIRS], BF16)
+        sin_bf16 = keep.tile([P, TOKEN_TILES, PAIRS], BF16)
+        nc.sync.dma_start(out=cos_bf16[:], in_=freqs_cos.rearrange("(m p) j -> p m j", p=P))
+        nc.sync.dma_start(out=sin_bf16[:], in_=freqs_sin.rearrange("(m p) j -> p m j", p=P))
+
+        gain = keep.tile([P, DIM], BF16)
+        for pair in range(PASSES // 2):
+            spread = bank_pool.tile([P, 2 * K_PASS], BF16, tag="bank")
+            for half in range(2):
+                c = 2 * pair + half
+                nc.tensor.matmul(
+                    out=spread[:, K_PASS * half : K_PASS * (half + 1)],
+                    lhsT=ident_bf16[:, c : c + 1].to_broadcast([P, P]),
+                    rhs=gain_rows[:],
+                    start=True,
+                    stop=True,
+                )
+            columns = slice(2 * K_PASS * pair, 2 * K_PASS * (pair + 1))
+            if pair % 2 == 0:
+                nc.scalar.copy(out=gain[:, columns], in_=spread[:])
+            else:
+                nc.vector.tensor_copy(out=gain[:, columns], in_=spread[:])
+
+        cos_pair = keep.tile([P, TOKEN_TILES, PAIRS, 2], F32)
+        nc.vector.tensor_copy(
+            out=cos_pair[:], in_=cos_bf16[:].unsqueeze(3).to_broadcast([P, TOKEN_TILES, PAIRS, 2])
+        )
+        sin_plus = keep.tile([P, TOKEN_TILES, PAIRS], F32)
+        nc.vector.tensor_copy(out=sin_plus[:], in_=sin_bf16[:])
+        sin_minus = keep.tile([P, TOKEN_TILES, PAIRS], F32)
+        nc.vector.tensor_scalar_mul(out=sin_minus[:], in0=sin_bf16[:], scalar1=-1.0)
+
+        def square_on_scalar(m, r):
+            scrap = scrap_pool.tile([P, RUN_K], BF16)
+            nc.scalar.activation(
+                out=scrap[:],
+                in_=x_pieces[(m, r)][:],
+                func=ACT.Square,
+                scale=1.0 / 128.0,
+                accum_out=sums[:, m, r : r + 1],
+            )
+
+        def square_on_vector(m, r):
+            scrap = h_pool.tile([P, RUN_K], BF16, tag="h")
+            nc.vector.scalar_tensor_tensor(
+                out=scrap[:],
+                in0=x_pieces[(m, r)][:],
+                scalar=1.0 / DIM,
+                in1=x_pieces[(m, r)][:],
+                op0=ALU.mult,
+                op1=ALU.mult,
+                accum_out=sums[:, m, 8 + r : 9 + r],
+            )
+
+        def finish_rstd(m):
+            mean_sq = small_pool.tile([P, 1], F32)
+            nc.vector.tensor_reduce(out=mean_sq[:], in_=sums[:, m, :], axis=AXIS.X, op=ALU.add)
+            rms = small_pool.tile([P, 1], F32)
+            nc.scalar.activation(out=rms[:], in_=mean_sq[:], func=ACT.Sqrt, bias=eps_col[:], scale=1.0)
+            nc.vector.reciprocal(out=rstd[:, m : m + 1], in_=rms[:])
+
+        def normalise(m, r):
+            h = h_pool.tile([P, RUN_K], BF16, tag="h")
+            nc.vector.scalar_tensor_tensor(
+                out=h[:],
+                in0=x_pieces[(m, r)][:],
+                scalar=rstd[:, m : m + 1],
+                in1=gain[:, RUN_K * r : RUN_K * (r + 1)],
+                op0=ALU.mult,
+                op1=ALU.mult,
+            )
+            return h
+
+        def transpose_and_regroup(h):
+            h_words = h[:].bitcast(F32)
+            grouped = grouped_pool.tile([P, RUN, P, 4], BF16, align_bytes=64)
+            grouped_words = (
+                grouped[:]
+                .rearrange("p g j t -> p (g j t)")
+                .bitcast(F32)
+                .rearrange("p (g j u) -> p g j u", g=RUN, u=2)
+            )
+            for b in range(RUN // 2):
+                bank = bank_pool.tile([P, 2, 2, P], F32, tag="bank")
+                for g in range(2):
+                    for u in range(2):
+                        first = (K_PASS // 2) * (2 * b + g)
+                        nc.tensor.transpose(
+                            out=bank[:, g, u, :],
+                            in_=h_words[:, first + u : first + K_PASS // 2 : 2],
+                            identity=ident_f32[:],
+                        )
+                nc.scalar.copy(
+                    out=grouped_words[:, 2 * b : 2 * b + 2], in_=bank[:].rearrange("p g u j -> p g j u")
+                )
+            return grouped
+
+        def quantise(grouped):
+            codes = code_pool.tile([P, RUN * P], U32, align_bytes=64)
+            plane = code_pool.tile([P, RUN * P], U8, align_bytes=64)
+            nc.vector.quantize_mx(
+                out=codes[:].bitcast(FP8X4), scales=plane[:], in_=grouped[:].rearrange("p g j t -> p (g j t)")
+            )
+            return codes, plane
+
+        def project(r, codes, plane, acc):
+            for g in range(RUN):
+                k_pass = RUN * r + g
+                tokens = slice(P * g, P * (g + 1))
+                nc.tensor.matmul_mx(
+                    out=acc[:],
+                    lhsT=codes[:, tokens].bitcast(FP8X4),
+                    lhsT_scale=plane[:, tokens],
+                    rhs=w_words[:, k_pass, :].bitcast(FP8X4),
+                    rhs_scale=w_planes[:, k_pass, :],
+                    start=(k_pass == 0),
+                    stop=(k_pass == PASSES - 1),
+                )
+
+        def rope_and_store(m, acc):
+            rows = slice(P * m, P * (m + 1))
+            qkv = out_pool.tile([P, N_OUT], F32)
+            nc.scalar.copy(out=qkv[:], in_=acc[:])
+            pairs = qkv[:, 0:N_ROPE].rearrange("p (h j e) -> p h j e", h=HEADS, e=2)
+            own = rope_pool.tile([P, HEADS, PAIRS, 2], F32)
+            nc.vector.tensor_tensor(
+                out=own[:],
+                in0=pairs,
+                in1=cos_pair[:, m].unsqueeze(1).to_broadcast([P, HEADS, PAIRS, 2]),
+                op=ALU.mult,
+            )
+            other = rope_pool.tile([P, 2, HEADS, PAIRS], F32)
+            nc.vector.tensor_tensor(
+                out=other[:, 0],
+                in0=pairs[:, :, :, 1],
+                in1=sin_minus[:, m].unsqueeze(1).to_broadcast([P, HEADS, PAIRS]),
+                op=ALU.mult,
+            )
+            nc.vector.tensor_tensor(
+                out=other[:, 1],
+                in0=pairs[:, :, :, 0],
+                in1=sin_plus[:, m].unsqueeze(1).to_broadcast([P, HEADS, PAIRS]),
+                op=ALU.mult,
+            )
+            rotated = out_pool.tile([P, N_ROPE], F32)
+            nc.vector.tensor_tensor(
+                out=rotated[:].rearrange("p (n e) -> p n e", e=2),
+                in0=own[:].rearrange("p h j e -> p (h j) e"),
+                in1=other[:].rearrange("p e h j -> p (h j) e"),
+                op=ALU.add,
+            )
+            nc.sync.dma_start(out=out_0[rows].rearrange("t h d -> t (h d)"), in_=rotated[:, 0:N_Q])
+            nc.sync.dma_start(out=out_1[rows].rearrange("t h d -> t (h d)"), in_=rotated[:, N_Q:N_ROPE])
+            nc.sync.dma_start(out=out_2[rows].rearrange("t h d -> t (h d)"), in_=qkv[:, N_ROPE:N_OUT])
+
+        for r in range(RUNS):
+            if r % 2 == 0:
+                square_on_scalar(0, r)
+            else:
+                square_on_vector(0, r)
+        finish_rstd(0)
+
+        for m in range(TOKEN_TILES):
+            acc = acc_pool.tile([P, N_OUT], F32)
+            for r in range(RUNS):
+                h = normalise(m, r)
+                if m + 2 < TOKEN_TILES:
+                    load_x(m + 2, r)
+                if m + 1 < TOKEN_TILES:
+                    square_on_scalar(m + 1, r)
+                grouped = transpose_and_regroup(h)
+                codes, plane = quantise(grouped)
+                project(r, codes, plane, acc)
+            if m + 1 < TOKEN_TILES:
+                finish_rstd(m + 1)
+            rope_and_store(m, acc)

@@ -29,6 +29,9 @@ N_ROPE = N_Q + N_K
 HEADS = N_ROPE // 32
 PAIRS = 16
 W_BLOCK = 8
+ALL_RUNS = TOKEN_TILES * RUNS
+LAG = 2
+SQUARES_AHEAD = RUNS + 1
 
 FLOPS = 2 * TOKENS * DIM * N_OUT
 
@@ -55,25 +58,28 @@ def tile_transformerblock_pa_k_kernel(
     with ExitStack() as stack:
         keep = stack.enter_context(tc.tile_pool(name="keep", bufs=1))
         x_pool = stack.enter_context(tc.tile_pool(name="x_pool", bufs=2 * RUNS))
-        h_pool = stack.enter_context(tc.tile_pool(name="h_pool", bufs=2))
-        grouped_pool = stack.enter_context(tc.tile_pool(name="grouped_pool", bufs=2))
-        code_pool = stack.enter_context(tc.tile_pool(name="code_pool", bufs=6))
+        h_pool = stack.enter_context(tc.tile_pool(name="h_pool", bufs=3))
+        grouped_pool = stack.enter_context(tc.tile_pool(name="grouped_pool", bufs=3))
+        code_pool = stack.enter_context(tc.tile_pool(name="code_pool", bufs=5))
         scrap_pool = stack.enter_context(tc.tile_pool(name="scrap_pool", bufs=1))
         small_pool = stack.enter_context(tc.tile_pool(name="small_pool", bufs=2))
         out_pool = stack.enter_context(tc.tile_pool(name="out_pool", bufs=2))
         rope_pool = stack.enter_context(tc.tile_pool(name="rope_pool", bufs=1))
         bank_pool = stack.enter_context(tc.psum_pool(name="bank_pool", bufs=6))
         acc_pool = stack.enter_context(tc.psum_pool(name="acc_pool", bufs=2))
+        stack.enter_context(tc.manual_schedule())
 
+        gain_rows = keep.tile([P, K_PASS], BF16)
+        nc.vector.memset(gain_rows[:], 0.0)
         eps_col = keep.tile([P, 1], F32)
         nc.vector.memset(eps_col[:], EPS)
         warm = keep.tile([P, 1], F32)
         nc.scalar.activation(out=warm[:], in_=eps_col[:], func=ACT.Sqrt)
 
-        ident_f32 = keep.tile([P, P], F32)
-        make_identity(nc, ident_f32[:])
         ident_bf16 = keep.tile([P, P], BF16)
         make_identity(nc, ident_bf16[:])
+        ident_f32 = keep.tile([P, P], F32)
+        make_identity(nc, ident_f32[:])
 
         sums = keep.tile([P, TOKEN_TILES, 16], F32)
         nc.vector.memset(sums[:], 0.0)
@@ -89,20 +95,24 @@ def tile_transformerblock_pa_k_kernel(
                     in_=scales[:, 4 * quadrant : 4 * quadrant + 4, :].rearrange("g q n -> q g n").bitcast(F32),
                 )
 
-        gain_rows = keep.tile([P, K_PASS], BF16)
-        nc.vector.memset(gain_rows[:], 0.0)
         nc.sync.dma_start(out=gain_rows[0:PASSES, :], in_=attn_norm_w.rearrange("(c n) -> c n", n=K_PASS))
 
         x_pieces = {}
 
-        def load_x(m, r):
+        def load_x(piece_index):
+            m, r = divmod(piece_index, RUNS)
             piece = x_pool.tile([P, RUN_K], BF16)
             nc.sync.dma_start(out=piece[:], in_=x[P * m : P * (m + 1), RUN_K * r : RUN_K * (r + 1)])
-            x_pieces[(m, r)] = piece
+            x_pieces[piece_index] = piece
 
-        for m in range(2):
-            for r in range(RUNS):
-                load_x(m, r)
+        for piece_index in range(RUNS):
+            load_x(piece_index)
+        cos_bf16 = keep.tile([P, TOKEN_TILES, PAIRS], BF16)
+        sin_bf16 = keep.tile([P, TOKEN_TILES, PAIRS], BF16)
+        nc.sync.dma_start(out=cos_bf16[:], in_=freqs_cos.rearrange("(m p) j -> p m j", p=P))
+        nc.sync.dma_start(out=sin_bf16[:], in_=freqs_sin.rearrange("(m p) j -> p m j", p=P))
+        for piece_index in range(RUNS, 2 * RUNS):
+            load_x(piece_index)
 
         for block in range(PASSES // W_BLOCK):
             passes = slice(W_BLOCK * block, W_BLOCK * (block + 1))
@@ -112,13 +122,9 @@ def tile_transformerblock_pa_k_kernel(
                     in_=words[passes].rearrange("g p n t -> p g (n t)").bitcast(I32),
                 )
 
-        cos_bf16 = keep.tile([P, TOKEN_TILES, PAIRS], BF16)
-        sin_bf16 = keep.tile([P, TOKEN_TILES, PAIRS], BF16)
-        nc.sync.dma_start(out=cos_bf16[:], in_=freqs_cos.rearrange("(m p) j -> p m j", p=P))
-        nc.sync.dma_start(out=sin_bf16[:], in_=freqs_sin.rearrange("(m p) j -> p m j", p=P))
-
         gain = keep.tile([P, DIM], BF16)
-        for pair in range(PASSES // 2):
+
+        def spread_gain(pair, engine_copy):
             spread = bank_pool.tile([P, 2 * K_PASS], BF16, tag="bank")
             for half in range(2):
                 c = 2 * pair + half
@@ -129,55 +135,48 @@ def tile_transformerblock_pa_k_kernel(
                     start=True,
                     stop=True,
                 )
-            columns = slice(2 * K_PASS * pair, 2 * K_PASS * (pair + 1))
-            if pair % 2 == 0:
-                nc.scalar.copy(out=gain[:, columns], in_=spread[:])
-            else:
-                nc.vector.tensor_copy(out=gain[:, columns], in_=spread[:])
+            engine_copy(out=gain[:, 2 * K_PASS * pair : 2 * K_PASS * (pair + 1)], in_=spread[:])
 
-        cos_pair = keep.tile([P, TOKEN_TILES, PAIRS, 2], F32)
-        nc.vector.tensor_copy(
-            out=cos_pair[:], in_=cos_bf16[:].unsqueeze(3).to_broadcast([P, TOKEN_TILES, PAIRS, 2])
-        )
-        sin_plus = keep.tile([P, TOKEN_TILES, PAIRS], F32)
-        nc.vector.tensor_copy(out=sin_plus[:], in_=sin_bf16[:])
-        sin_minus = keep.tile([P, TOKEN_TILES, PAIRS], F32)
-        nc.vector.tensor_scalar_mul(out=sin_minus[:], in0=sin_bf16[:], scalar1=-1.0)
-
-        def square_on_scalar(m, r):
+        def square_on_scalar(piece_index):
+            m, r = divmod(piece_index, RUNS)
             scrap = scrap_pool.tile([P, RUN_K], BF16)
             nc.scalar.activation(
                 out=scrap[:],
-                in_=x_pieces[(m, r)][:],
+                in_=x_pieces[piece_index][:],
                 func=ACT.Square,
                 scale=1.0 / 128.0,
                 accum_out=sums[:, m, r : r + 1],
             )
 
-        def square_on_vector(m, r):
+        def square_on_vector(piece_index):
+            m, r = divmod(piece_index, RUNS)
             scrap = h_pool.tile([P, RUN_K], BF16, tag="h")
             nc.vector.scalar_tensor_tensor(
                 out=scrap[:],
-                in0=x_pieces[(m, r)][:],
+                in0=x_pieces[piece_index][:],
                 scalar=1.0 / DIM,
-                in1=x_pieces[(m, r)][:],
+                in1=x_pieces[piece_index][:],
                 op0=ALU.mult,
                 op1=ALU.mult,
                 accum_out=sums[:, m, 8 + r : 9 + r],
             )
 
-        def finish_rstd(m):
+        def root_mean_square(m):
             mean_sq = small_pool.tile([P, 1], F32)
             nc.vector.tensor_reduce(out=mean_sq[:], in_=sums[:, m, :], axis=AXIS.X, op=ALU.add)
             rms = small_pool.tile([P, 1], F32)
             nc.scalar.activation(out=rms[:], in_=mean_sq[:], func=ACT.Sqrt, bias=eps_col[:], scale=1.0)
+            return rms
+
+        def invert(m, rms):
             nc.vector.reciprocal(out=rstd[:, m : m + 1], in_=rms[:])
 
-        def normalise(m, r):
+        def normalise(s):
+            m, r = divmod(s, RUNS)
             h = h_pool.tile([P, RUN_K], BF16, tag="h")
             nc.vector.scalar_tensor_tensor(
                 out=h[:],
-                in0=x_pieces[(m, r)][:],
+                in0=x_pieces[s][:],
                 scalar=rstd[:, m : m + 1],
                 in1=gain[:, RUN_K * r : RUN_K * (r + 1)],
                 op0=ALU.mult,
@@ -194,6 +193,7 @@ def tile_transformerblock_pa_k_kernel(
                 .bitcast(F32)
                 .rearrange("p (g j u) -> p g j u", g=RUN, u=2)
             )
+            banks = []
             for b in range(RUN // 2):
                 bank = bank_pool.tile([P, 2, 2, P], F32, tag="bank")
                 for g in range(2):
@@ -204,8 +204,10 @@ def tile_transformerblock_pa_k_kernel(
                             in_=h_words[:, first + u : first + K_PASS // 2 : 2],
                             identity=ident_f32[:],
                         )
+                banks.append(bank)
+            for b in range(RUN // 2):
                 nc.scalar.copy(
-                    out=grouped_words[:, 2 * b : 2 * b + 2], in_=bank[:].rearrange("p g u j -> p g j u")
+                    out=grouped_words[:, 2 * b : 2 * b + 2], in_=banks[b][:].rearrange("p g u j -> p g j u")
                 )
             return grouped
 
@@ -231,10 +233,13 @@ def tile_transformerblock_pa_k_kernel(
                     stop=(k_pass == PASSES - 1),
                 )
 
-        def rope_and_store(m, acc):
-            rows = slice(P * m, P * (m + 1))
+        def collect(acc):
             qkv = out_pool.tile([P, N_OUT], F32)
             nc.scalar.copy(out=qkv[:], in_=acc[:])
+            return qkv
+
+        def rope_and_store(m, qkv):
+            rows = slice(P * m, P * (m + 1))
             pairs = qkv[:, 0:N_ROPE].rearrange("p (h j e) -> p h j e", h=HEADS, e=2)
             own = rope_pool.tile([P, HEADS, PAIRS, 2], F32)
             nc.vector.tensor_tensor(
@@ -267,24 +272,50 @@ def tile_transformerblock_pa_k_kernel(
             nc.sync.dma_start(out=out_1[rows].rearrange("t h d -> t (h d)"), in_=rotated[:, N_Q:N_ROPE])
             nc.sync.dma_start(out=out_2[rows].rearrange("t h d -> t (h d)"), in_=qkv[:, N_ROPE:N_OUT])
 
-        for r in range(RUNS):
-            if r % 2 == 0:
-                square_on_scalar(0, r)
+        for piece_index in range(SQUARES_AHEAD):
+            if piece_index < RUNS:
+                spread_gain(2 * piece_index, nc.scalar.copy)
+                spread_gain(2 * piece_index + 1, nc.vector.tensor_copy)
+            if piece_index % 2 == 0:
+                square_on_scalar(piece_index)
             else:
-                square_on_vector(0, r)
-        finish_rstd(0)
+                square_on_vector(piece_index)
 
-        for m in range(TOKEN_TILES):
-            acc = acc_pool.tile([P, N_OUT], F32)
-            for r in range(RUNS):
-                h = normalise(m, r)
-                if m + 2 < TOKEN_TILES:
-                    load_x(m + 2, r)
-                if m + 1 < TOKEN_TILES:
-                    square_on_scalar(m + 1, r)
-                grouped = transpose_and_regroup(h)
-                codes, plane = quantise(grouped)
-                project(r, codes, plane, acc)
-            if m + 1 < TOKEN_TILES:
-                finish_rstd(m + 1)
-            rope_and_store(m, acc)
+        cos_pair = keep.tile([P, TOKEN_TILES, PAIRS, 2], F32)
+        nc.vector.tensor_copy(
+            out=cos_pair[:], in_=cos_bf16[:].unsqueeze(3).to_broadcast([P, TOKEN_TILES, PAIRS, 2])
+        )
+        sin_plus = keep.tile([P, TOKEN_TILES, PAIRS], F32)
+        nc.vector.tensor_copy(out=sin_plus[:], in_=sin_bf16[:])
+        sin_minus = keep.tile([P, TOKEN_TILES, PAIRS], F32)
+        nc.vector.tensor_scalar_mul(out=sin_minus[:], in0=sin_bf16[:], scalar1=-1.0)
+        invert(0, root_mean_square(0))
+
+        grouped_of = {}
+        acc_of = {}
+        qkv_of = {}
+        for s in range(ALL_RUNS + LAG + 1):
+            next_tile_is_near = s % RUNS == RUNS - 1 and s + 1 < ALL_RUNS
+            if next_tile_is_near:
+                rms = root_mean_square((s + 1) // RUNS)
+            if s < ALL_RUNS:
+                h = normalise(s)
+                if s + 2 * RUNS < ALL_RUNS:
+                    load_x(s + 2 * RUNS)
+                if s + SQUARES_AHEAD < ALL_RUNS:
+                    square_on_scalar(s + SQUARES_AHEAD)
+                grouped_of[s] = transpose_and_regroup(h)
+            late = s - LAG
+            if 0 <= late < ALL_RUNS:
+                m, r = divmod(late, RUNS)
+                if r == 0:
+                    acc_of[m] = acc_pool.tile([P, N_OUT], F32, name="acc")
+                codes, plane = quantise(grouped_of[late])
+                project(r, codes, plane, acc_of[m])
+                if r == RUNS - 1:
+                    qkv_of[m] = collect(acc_of[m])
+            if next_tile_is_near:
+                invert((s + 1) // RUNS, rms)
+            done = s - LAG - 1
+            if done >= 0 and done % RUNS == RUNS - 1:
+                rope_and_store(done // RUNS, qkv_of[done // RUNS])

@@ -137,6 +137,10 @@ def tile_transformerblock_pa_k_kernel(
                 )
             engine_copy(out=gain[:, 2 * K_PASS * pair : 2 * K_PASS * (pair + 1)], in_=spread[:])
 
+        def spread_gain_for_run(r):
+            spread_gain(2 * r, nc.scalar.copy)
+            spread_gain(2 * r + 1, nc.vector.tensor_copy)
+
         def square_on_scalar(piece_index):
             m, r = divmod(piece_index, RUNS)
             scrap = scrap_pool.tile([P, RUN_K], BF16)
@@ -184,15 +188,8 @@ def tile_transformerblock_pa_k_kernel(
             )
             return h
 
-        def transpose_and_regroup(h):
+        def transpose(h):
             h_words = h[:].bitcast(F32)
-            grouped = grouped_pool.tile([P, RUN, P, 4], BF16, align_bytes=64)
-            grouped_words = (
-                grouped[:]
-                .rearrange("p g j t -> p (g j t)")
-                .bitcast(F32)
-                .rearrange("p (g j u) -> p g j u", g=RUN, u=2)
-            )
             banks = []
             for b in range(RUN // 2):
                 bank = bank_pool.tile([P, 2, 2, P], F32, tag="bank")
@@ -205,10 +202,19 @@ def tile_transformerblock_pa_k_kernel(
                             identity=ident_f32[:],
                         )
                 banks.append(bank)
+            return banks
+
+        def regroup(banks, vector_helps):
+            grouped = grouped_pool.tile([P, RUN, P, 4], BF16, align_bytes=64)
+            grouped_words = (
+                grouped[:]
+                .rearrange("p g j t -> p (g j t)")
+                .bitcast(F32)
+                .rearrange("p (g j u) -> p g j u", g=RUN, u=2)
+            )
             for b in range(RUN // 2):
-                nc.scalar.copy(
-                    out=grouped_words[:, 2 * b : 2 * b + 2], in_=banks[b][:].rearrange("p g u j -> p g j u")
-                )
+                copy_out = nc.vector.tensor_copy if vector_helps and b == RUN // 2 - 1 else nc.scalar.copy
+                copy_out(out=grouped_words[:, 2 * b : 2 * b + 2], in_=banks[b][:].rearrange("p g u j -> p g j u"))
             return grouped
 
         def quantise(grouped):
@@ -272,10 +278,8 @@ def tile_transformerblock_pa_k_kernel(
             nc.sync.dma_start(out=out_1[rows].rearrange("t h d -> t (h d)"), in_=rotated[:, N_Q:N_ROPE])
             nc.sync.dma_start(out=out_2[rows].rearrange("t h d -> t (h d)"), in_=qkv[:, N_ROPE:N_OUT])
 
-        for piece_index in range(SQUARES_AHEAD):
-            if piece_index < RUNS:
-                spread_gain(2 * piece_index, nc.scalar.copy)
-                spread_gain(2 * piece_index + 1, nc.vector.tensor_copy)
+        spread_gain_for_run(0)
+        for piece_index in range(RUNS):
             if piece_index % 2 == 0:
                 square_on_scalar(piece_index)
             else:
@@ -290,7 +294,10 @@ def tile_transformerblock_pa_k_kernel(
         sin_minus = keep.tile([P, TOKEN_TILES, PAIRS], F32)
         nc.vector.tensor_scalar_mul(out=sin_minus[:], in0=sin_bf16[:], scalar1=-1.0)
         invert(0, root_mean_square(0))
+        for piece_index in range(RUNS, SQUARES_AHEAD):
+            square_on_scalar(piece_index)
 
+        banks_of = {}
         grouped_of = {}
         acc_of = {}
         qkv_of = {}
@@ -302,9 +309,13 @@ def tile_transformerblock_pa_k_kernel(
                 h = normalise(s)
                 if s + 2 * RUNS < ALL_RUNS:
                     load_x(s + 2 * RUNS)
+                if s + 1 < RUNS:
+                    spread_gain_for_run(s + 1)
                 if s + SQUARES_AHEAD < ALL_RUNS:
                     square_on_scalar(s + SQUARES_AHEAD)
-                grouped_of[s] = transpose_and_regroup(h)
+                banks_of[s] = transpose(h)
+            if 0 <= s - 1 < ALL_RUNS:
+                grouped_of[s - 1] = regroup(banks_of[s - 1], s % 3 == 1 and s + SQUARES_AHEAD < ALL_RUNS)
             late = s - LAG
             if 0 <= late < ALL_RUNS:
                 m, r = divmod(late, RUNS)

@@ -278,8 +278,8 @@ def tile_transformerblock_pa_k_kernel(
             nc.sync.dma_start(out=out_1[rows].rearrange("t h d -> t (h d)"), in_=rotated[:, N_Q:N_ROPE])
             nc.sync.dma_start(out=out_2[rows].rearrange("t h d -> t (h d)"), in_=qkv[:, N_ROPE:N_OUT])
 
-        spread_gain_for_run(0)
         for piece_index in range(RUNS):
+            spread_gain_for_run(piece_index)
             if piece_index % 2 == 0:
                 square_on_scalar(piece_index)
             else:
@@ -309,8 +309,6 @@ def tile_transformerblock_pa_k_kernel(
                 h = normalise(s)
                 if s + 2 * RUNS < ALL_RUNS:
                     load_x(s + 2 * RUNS)
-                if s + 1 < RUNS:
-                    spread_gain_for_run(s + 1)
                 if s + SQUARES_AHEAD < ALL_RUNS:
                     square_on_scalar(s + SQUARES_AHEAD)
                 banks_of[s] = transpose(h)

@@ -17,21 +17,24 @@ P = 128
 TOKENS = 512
 DIM = 16384
 EPS = 1e-6
+HALF = DIM // 2
+GROUP = P // 2
+GROUPS = TOKENS // GROUP
 TOKEN_TILES = TOKENS // P
 K_PASS = 4 * P
 PASSES = DIM // K_PASS
-RUN = 4
-RUN_K = RUN * K_PASS
-RUNS = PASSES // RUN
+RUN_K = 4 * K_PASS
+RUN = RUN_K // K_PASS
+RUNS = HALF // RUN_K
+ALL_RUNS = GROUPS * RUNS
+CHUNKS = HALF // K_PASS
 N_Q, N_K, N_V = 256, 128, 128
 N_OUT = N_Q + N_K + N_V
 N_ROPE = N_Q + N_K
 HEADS = N_ROPE // 32
 PAIRS = 16
-W_BLOCK = 8
-ALL_RUNS = TOKEN_TILES * RUNS
-LAG = 2
-SQUARES_AHEAD = RUNS + 1
+SQUARES_AHEAD = RUNS + 2
+PASSES_A_STEP = 5
 
 FLOPS = 2 * TOKENS * DIM * N_OUT
 
@@ -57,10 +60,10 @@ def tile_transformerblock_pa_k_kernel(
 
     with ExitStack() as stack:
         keep = stack.enter_context(tc.tile_pool(name="keep", bufs=1))
-        x_pool = stack.enter_context(tc.tile_pool(name="x_pool", bufs=2 * RUNS))
+        x_pool = stack.enter_context(tc.tile_pool(name="x_pool", bufs=12))
         h_pool = stack.enter_context(tc.tile_pool(name="h_pool", bufs=3))
-        grouped_pool = stack.enter_context(tc.tile_pool(name="grouped_pool", bufs=3))
-        code_pool = stack.enter_context(tc.tile_pool(name="code_pool", bufs=5))
+        grouped_pool = stack.enter_context(tc.tile_pool(name="grouped_pool", bufs=RUNS + 1))
+        code_pool = stack.enter_context(tc.tile_pool(name="code_pool", bufs=4))
         scrap_pool = stack.enter_context(tc.tile_pool(name="scrap_pool", bufs=1))
         small_pool = stack.enter_context(tc.tile_pool(name="small_pool", bufs=2))
         out_pool = stack.enter_context(tc.tile_pool(name="out_pool", bufs=2))
@@ -71,23 +74,54 @@ def tile_transformerblock_pa_k_kernel(
 
         gain_rows = keep.tile([P, K_PASS], BF16)
         nc.vector.memset(gain_rows[:], 0.0)
+        nc.sync.dma_start(out=gain_rows[0:PASSES, :], in_=attn_norm_w.rearrange("(c n) -> c n", n=K_PASS))
+
+        x_halves = x.rearrange("t (h k) -> (t h) k", h=2)
+        x_pieces = {}
+
+        def load_x(s):
+            g, c = divmod(s, RUNS)
+            piece = x_pool.tile([P, RUN_K], BF16)
+            nc.sync.dma_start(out=piece[:], in_=x_halves[P * g : P * (g + 1), RUN_K * c : RUN_K * (c + 1)])
+            x_pieces[s] = piece
+
+        for s in range(2 * RUNS):
+            load_x(s)
+        cos_bf16 = keep.tile([P, TOKEN_TILES, PAIRS], BF16)
+        sin_bf16 = keep.tile([P, TOKEN_TILES, PAIRS], BF16)
+        nc.sync.dma_start(out=cos_bf16[:], in_=freqs_cos.rearrange("(m p) j -> p m j", p=P))
+        nc.sync.dma_start(out=sin_bf16[:], in_=freqs_sin.rearrange("(m p) j -> p m j", p=P))
+        for s in range(2 * RUNS, 3 * RUNS):
+            load_x(s)
+
+        w_words = keep.tile([P, PASSES, N_OUT], I32, align_bytes=64)
+
+        def load_weights(first_pass):
+            passes = slice(first_pass, first_pass + RUN)
+            for words, unused_scales, first, width in weights:
+                nc.sync.dma_start(
+                    out=w_words[:, passes, first : first + width],
+                    in_=words[passes].rearrange("g p n t -> p g (n t)").bitcast(I32),
+                )
+
+        for c in range(RUNS):
+            for h in range(2):
+                load_weights(CHUNKS * h + RUN * c)
+
         eps_col = keep.tile([P, 1], F32)
         nc.vector.memset(eps_col[:], EPS)
         warm = keep.tile([P, 1], F32)
         nc.scalar.activation(out=warm[:], in_=eps_col[:], func=ACT.Sqrt)
 
-        ident_bf16 = keep.tile([P, P], BF16)
-        make_identity(nc, ident_bf16[:])
-        ident_f32 = keep.tile([P, P], F32)
-        make_identity(nc, ident_f32[:])
-
-        sums = keep.tile([P, TOKEN_TILES, 16], F32)
+        sums = keep.tile([P, GROUPS, 2 * RUNS], F32)
         nc.vector.memset(sums[:], 0.0)
-        rstd = keep.tile([P, TOKEN_TILES], F32)
+        rstd = keep.tile([P, GROUPS], F32)
 
-        w_words = keep.tile([P, PASSES, N_OUT], I32, align_bytes=64)
+        ident = keep.tile([P, P], F32)
+        make_identity(nc, ident[:])
+
         w_planes = keep.tile([P, PASSES, N_OUT], U8, align_bytes=64)
-        nc.vector.memset(w_planes[:].rearrange("p g n -> p (g n)").bitcast(I32), 0)
+        nc.gpsimd.memset(w_planes[:].rearrange("p g n -> p (g n)").bitcast(I32), 0)
         for quadrant in range(4):
             for unused_words, scales, first, width in weights:
                 nc.gpsimd.dma_start(
@@ -95,94 +129,94 @@ def tile_transformerblock_pa_k_kernel(
                     in_=scales[:, 4 * quadrant : 4 * quadrant + 4, :].rearrange("g q n -> q g n").bitcast(F32),
                 )
 
-        nc.sync.dma_start(out=gain_rows[0:PASSES, :], in_=attn_norm_w.rearrange("(c n) -> c n", n=K_PASS))
+        select = keep.tile([P, CHUNKS, GROUP, 2], BF16)
+        nc.vector.tensor_copy(
+            out=select[:],
+            in_=ident[:, 0:PASSES]
+            .rearrange("k (h c) -> k c h", h=2)
+            .unsqueeze(2)
+            .to_broadcast([P, CHUNKS, GROUP, 2]),
+        )
+        by_half = ident[:].rearrange("k (t h) -> k h t", h=2)
+        permute = keep.tile([P, 2, GROUP], F32)
+        nc.vector.tensor_copy(out=permute[:], in_=by_half)
+        both = keep.tile([P, GROUP, 2], F32)
+        nc.vector.tensor_tensor(
+            out=both[:],
+            in0=by_half[:, 0].unsqueeze(2).to_broadcast([P, GROUP, 2]),
+            in1=by_half[:, 1].unsqueeze(2).to_broadcast([P, GROUP, 2]),
+            op=ALU.add,
+        )
+        gain = keep.tile([P, HALF], BF16)
 
-        x_pieces = {}
-
-        def load_x(piece_index):
-            m, r = divmod(piece_index, RUNS)
-            piece = x_pool.tile([P, RUN_K], BF16)
-            nc.sync.dma_start(out=piece[:], in_=x[P * m : P * (m + 1), RUN_K * r : RUN_K * (r + 1)])
-            x_pieces[piece_index] = piece
-
-        for piece_index in range(RUNS):
-            load_x(piece_index)
-        cos_bf16 = keep.tile([P, TOKEN_TILES, PAIRS], BF16)
-        sin_bf16 = keep.tile([P, TOKEN_TILES, PAIRS], BF16)
-        nc.sync.dma_start(out=cos_bf16[:], in_=freqs_cos.rearrange("(m p) j -> p m j", p=P))
-        nc.sync.dma_start(out=sin_bf16[:], in_=freqs_sin.rearrange("(m p) j -> p m j", p=P))
-        for piece_index in range(RUNS, 2 * RUNS):
-            load_x(piece_index)
-
-        for block in range(PASSES // W_BLOCK):
-            passes = slice(W_BLOCK * block, W_BLOCK * (block + 1))
-            for words, unused_scales, first, width in weights:
-                nc.sync.dma_start(
-                    out=w_words[:, passes, first : first + width],
-                    in_=words[passes].rearrange("g p n t -> p g (n t)").bitcast(I32),
-                )
-
-        gain = keep.tile([P, DIM], BF16)
-
-        def spread_gain(pair, engine_copy):
+        def spread_gain(pair):
             spread = bank_pool.tile([P, 2 * K_PASS], BF16, tag="bank")
             for half in range(2):
                 c = 2 * pair + half
                 nc.tensor.matmul(
                     out=spread[:, K_PASS * half : K_PASS * (half + 1)],
-                    lhsT=ident_bf16[:, c : c + 1].to_broadcast([P, P]),
+                    lhsT=select[:, c].rearrange("k t h -> k (t h)"),
                     rhs=gain_rows[:],
                     start=True,
                     stop=True,
                 )
-            engine_copy(out=gain[:, 2 * K_PASS * pair : 2 * K_PASS * (pair + 1)], in_=spread[:])
+            return spread
 
-        def spread_gain_for_run(r):
-            spread_gain(2 * r, nc.scalar.copy)
-            spread_gain(2 * r + 1, nc.vector.tensor_copy)
+        def keep_gain(pair, spread, copy_out):
+            copy_out(out=gain[:, 2 * K_PASS * pair : 2 * K_PASS * (pair + 1)], in_=spread[:])
 
-        def square_on_scalar(piece_index):
-            m, r = divmod(piece_index, RUNS)
+        def square_on_scalar(s):
+            g, c = divmod(s, RUNS)
             scrap = scrap_pool.tile([P, RUN_K], BF16)
             nc.scalar.activation(
                 out=scrap[:],
-                in_=x_pieces[piece_index][:],
+                in_=x_pieces[s][:],
                 func=ACT.Square,
                 scale=1.0 / 128.0,
-                accum_out=sums[:, m, r : r + 1],
+                accum_out=sums[:, g, c : c + 1],
             )
 
-        def square_on_vector(piece_index):
-            m, r = divmod(piece_index, RUNS)
+        def square_on_vector(s):
+            g, c = divmod(s, RUNS)
             scrap = h_pool.tile([P, RUN_K], BF16, tag="h")
             nc.vector.scalar_tensor_tensor(
                 out=scrap[:],
-                in0=x_pieces[piece_index][:],
+                in0=x_pieces[s][:],
                 scalar=1.0 / DIM,
-                in1=x_pieces[piece_index][:],
+                in1=x_pieces[s][:],
                 op0=ALU.mult,
                 op1=ALU.mult,
-                accum_out=sums[:, m, 8 + r : 9 + r],
+                accum_out=sums[:, g, RUNS + c : RUNS + c + 1],
             )
 
-        def root_mean_square(m):
-            mean_sq = small_pool.tile([P, 1], F32)
-            nc.vector.tensor_reduce(out=mean_sq[:], in_=sums[:, m, :], axis=AXIS.X, op=ALU.add)
+        def add_squares(g):
+            half_sum = small_pool.tile([P, 1], F32)
+            nc.vector.tensor_reduce(out=half_sum[:], in_=sums[:, g, :], axis=AXIS.X, op=ALU.add)
+            return half_sum
+
+        def add_halves(half_sum):
+            mean_sq = bank_pool.tile([P, 1], F32, tag="bank")
+            nc.tensor.matmul(
+                out=mean_sq[:], lhsT=both[:].rearrange("k t h -> k (t h)"), rhs=half_sum[:], start=True, stop=True
+            )
+            return mean_sq
+
+        def root(mean_sq):
             rms = small_pool.tile([P, 1], F32)
             nc.scalar.activation(out=rms[:], in_=mean_sq[:], func=ACT.Sqrt, bias=eps_col[:], scale=1.0)
             return rms
 
-        def invert(m, rms):
-            nc.vector.reciprocal(out=rstd[:, m : m + 1], in_=rms[:])
+        def invert(g, rms):
+            nc.vector.reciprocal(out=rstd[:, g : g + 1], in_=rms[:])
 
         def normalise(s):
-            m, r = divmod(s, RUNS)
+            g, c = divmod(s, RUNS)
             h = h_pool.tile([P, RUN_K], BF16, tag="h")
             nc.vector.scalar_tensor_tensor(
                 out=h[:],
                 in0=x_pieces[s][:],
-                scalar=rstd[:, m : m + 1],
-                in1=gain[:, RUN_K * r : RUN_K * (r + 1)],
+                scalar=rstd[:, g : g + 1],
+                in1=gain[:, RUN_K * c : RUN_K * (c + 1)],
                 op0=ALU.mult,
                 op1=ALU.mult,
             )
@@ -193,60 +227,84 @@ def tile_transformerblock_pa_k_kernel(
             banks = []
             for b in range(RUN // 2):
                 bank = bank_pool.tile([P, 2, 2, P], F32, tag="bank")
-                for g in range(2):
-                    for u in range(2):
-                        first = (K_PASS // 2) * (2 * b + g)
+                for u in range(2):
+                    for i in range(2):
+                        first = (K_PASS // 2) * (2 * b + i)
                         nc.tensor.transpose(
-                            out=bank[:, g, u, :],
+                            out=bank[:, u, i, :],
                             in_=h_words[:, first + u : first + K_PASS // 2 : 2],
-                            identity=ident_f32[:],
+                            identity=permute[:].rearrange("k h t -> k (h t)"),
                         )
                 banks.append(bank)
             return banks
 
-        def regroup(banks, vector_helps):
-            grouped = grouped_pool.tile([P, RUN, P, 4], BF16, align_bytes=64)
+        grouped_tiles = {}
+
+        def regroup(s, banks, vector_share):
+            g, c = divmod(s, RUNS)
+            m, part = divmod(g, 2)
+            if part == 0:
+                grouped_tiles[m, c] = grouped_pool.tile([P, 2 * RUN, P, 4], BF16, align_bytes=64, name="grouped")
             grouped_words = (
-                grouped[:]
-                .rearrange("p g j t -> p (g j t)")
+                grouped_tiles[m, c][:]
+                .rearrange("p i j t -> p (i j t)")
                 .bitcast(F32)
-                .rearrange("p (g j u) -> p g j u", g=RUN, u=2)
+                .rearrange("p (i j u) -> p i j u", i=2 * RUN, u=2)
             )
             for b in range(RUN // 2):
-                copy_out = nc.vector.tensor_copy if vector_helps and b == RUN // 2 - 1 else nc.scalar.copy
-                copy_out(out=grouped_words[:, 2 * b : 2 * b + 2], in_=banks[b][:].rearrange("p g u j -> p g j u"))
-            return grouped
-
-        def quantise(grouped):
-            codes = code_pool.tile([P, RUN * P], U32, align_bytes=64)
-            plane = code_pool.tile([P, RUN * P], U8, align_bytes=64)
-            nc.vector.quantize_mx(
-                out=codes[:].bitcast(FP8X4), scales=plane[:], in_=grouped[:].rearrange("p g j t -> p (g j t)")
-            )
-            return codes, plane
-
-        def project(r, codes, plane, acc):
-            for g in range(RUN):
-                k_pass = RUN * r + g
-                tokens = slice(P * g, P * (g + 1))
-                nc.tensor.matmul_mx(
-                    out=acc[:],
-                    lhsT=codes[:, tokens].bitcast(FP8X4),
-                    lhsT_scale=plane[:, tokens],
-                    rhs=w_words[:, k_pass, :].bitcast(FP8X4),
-                    rhs_scale=w_planes[:, k_pass, :],
-                    start=(k_pass == 0),
-                    stop=(k_pass == PASSES - 1),
+                copy_out = nc.vector.tensor_copy if b >= RUN // 2 - vector_share else nc.scalar.copy
+                copy_out(
+                    out=grouped_words[:, 4 * b : 4 * b + 4, GROUP * part : GROUP * (part + 1)],
+                    in_=banks[b][:].rearrange("p u i (h j) -> p (i h) j u", h=2),
                 )
 
-        def collect(acc):
-            qkv = out_pool.tile([P, N_OUT], F32)
-            nc.scalar.copy(out=qkv[:], in_=acc[:])
-            return qkv
+        waiting = []
 
-        def rope_and_store(m, qkv):
+        def quantise(m, c):
+            grouped = grouped_tiles[m, c]
+            codes = code_pool.tile([P, 2 * RUN * P], U32, align_bytes=64)
+            plane = code_pool.tile([P, 2 * RUN * P], U8, align_bytes=64)
+            nc.vector.quantize_mx(
+                out=codes[:].bitcast(FP8X4), scales=plane[:], in_=grouped[:].rearrange("p i j t -> p (i j t)")
+            )
+            for i in range(2 * RUN):
+                tokens = slice(P * i, P * (i + 1))
+                k_pass = CHUNKS * (i % 2) + RUN * c + i // 2
+                waiting.append((m, k_pass, c == 0 and i == 0, c == RUNS - 1 and i == 2 * RUN - 1, codes[:, tokens], plane[:, tokens]))
+
+        acc_of = {}
+
+        def project(m, k_pass, first, last, codes, plane):
+            if first:
+                acc_of[m] = acc_pool.tile([P, N_OUT], F32, name="acc")
+            nc.tensor.matmul_mx(
+                out=acc_of[m][:],
+                lhsT=codes.bitcast(FP8X4),
+                lhsT_scale=plane,
+                rhs=w_words[:, k_pass, :].bitcast(FP8X4),
+                rhs_scale=w_planes[:, k_pass, :],
+                start=first,
+                stop=last,
+            )
+
+        cos_pair = keep.tile([P, TOKEN_TILES, PAIRS, 2], F32)
+        sin_plus = keep.tile([P, TOKEN_TILES, PAIRS], F32)
+        sin_minus = keep.tile([P, TOKEN_TILES, PAIRS], F32)
+
+        def fill_rope_tables():
+            nc.vector.tensor_copy(
+                out=cos_pair[:], in_=cos_bf16[:].unsqueeze(3).to_broadcast([P, TOKEN_TILES, PAIRS, 2])
+            )
+            nc.vector.tensor_copy(out=sin_plus[:], in_=sin_bf16[:])
+            nc.vector.tensor_scalar_mul(out=sin_minus[:], in0=sin_bf16[:], scalar1=-1.0)
+
+        def rope_and_store(m):
             rows = slice(P * m, P * (m + 1))
-            pairs = qkv[:, 0:N_ROPE].rearrange("p (h j e) -> p h j e", h=HEADS, e=2)
+            acc = acc_of[m]
+            value = out_pool.tile([P, N_V], F32)
+            nc.scalar.copy(out=value[:], in_=acc[:, N_ROPE:N_OUT])
+            nc.sync.dma_start(out=out_2[rows].rearrange("t h d -> t (h d)"), in_=value[:])
+            pairs = acc[:, 0:N_ROPE].rearrange("p (h j e) -> p h j e", h=HEADS, e=2)
             own = rope_pool.tile([P, HEADS, PAIRS, 2], F32)
             nc.vector.tensor_tensor(
                 out=own[:],
@@ -276,55 +334,65 @@ def tile_transformerblock_pa_k_kernel(
             )
             nc.sync.dma_start(out=out_0[rows].rearrange("t h d -> t (h d)"), in_=rotated[:, 0:N_Q])
             nc.sync.dma_start(out=out_1[rows].rearrange("t h d -> t (h d)"), in_=rotated[:, N_Q:N_ROPE])
-            nc.sync.dma_start(out=out_2[rows].rearrange("t h d -> t (h d)"), in_=qkv[:, N_ROPE:N_OUT])
 
-        for piece_index in range(RUNS):
-            spread_gain_for_run(piece_index)
-            if piece_index % 2 == 0:
-                square_on_scalar(piece_index)
-            else:
-                square_on_vector(piece_index)
-
-        cos_pair = keep.tile([P, TOKEN_TILES, PAIRS, 2], F32)
-        nc.vector.tensor_copy(
-            out=cos_pair[:], in_=cos_bf16[:].unsqueeze(3).to_broadcast([P, TOKEN_TILES, PAIRS, 2])
-        )
-        sin_plus = keep.tile([P, TOKEN_TILES, PAIRS], F32)
-        nc.vector.tensor_copy(out=sin_plus[:], in_=sin_bf16[:])
-        sin_minus = keep.tile([P, TOKEN_TILES, PAIRS], F32)
-        nc.vector.tensor_scalar_mul(out=sin_minus[:], in0=sin_bf16[:], scalar1=-1.0)
-        invert(0, root_mean_square(0))
-        for piece_index in range(RUNS, SQUARES_AHEAD):
-            square_on_scalar(piece_index)
+        spreads = []
+        for pair in range(6):
+            spreads.append(spread_gain(pair))
+        keep_gain(0, spreads[0], nc.scalar.copy)
+        square_on_scalar(0)
+        square_on_vector(1)
+        square_on_scalar(2)
+        keep_gain(1, spreads[1], nc.vector.tensor_copy)
+        square_on_vector(3)
+        rms = root(add_halves(add_squares(0)))
+        keep_gain(3, spreads[3], nc.vector.tensor_copy)
+        keep_gain(4, spreads[4], nc.vector.tensor_copy)
+        invert(0, rms)
+        keep_gain(2, spreads[2], nc.scalar.copy)
+        for pair in range(6, 2 * RUNS):
+            spreads.append(spread_gain(pair))
+        for s in range(RUNS, SQUARES_AHEAD):
+            square_on_scalar(s)
 
         banks_of = {}
-        grouped_of = {}
-        acc_of = {}
-        qkv_of = {}
-        for s in range(ALL_RUNS + LAG + 1):
-            next_tile_is_near = s % RUNS == RUNS - 1 and s + 1 < ALL_RUNS
-            if next_tile_is_near:
-                rms = root_mean_square((s + 1) // RUNS)
+        to_rope = []
+        for s in range(ALL_RUNS + 1):
+            g, c = divmod(s, RUNS)
+            squares_left = s + SQUARES_AHEAD < ALL_RUNS
             if s < ALL_RUNS:
                 h = normalise(s)
-                if s + 2 * RUNS < ALL_RUNS:
-                    load_x(s + 2 * RUNS)
-                if s + SQUARES_AHEAD < ALL_RUNS:
+                if s + 3 * RUNS < ALL_RUNS:
+                    load_x(s + 3 * RUNS)
+                if squares_left:
                     square_on_scalar(s + SQUARES_AHEAD)
                 banks_of[s] = transpose(h)
+            if s == 0:
+                keep_gain(5, spreads[5], nc.vector.tensor_copy)
+            if s == 1:
+                keep_gain(6, spreads[6], nc.vector.tensor_copy)
+                keep_gain(7, spreads[7], nc.vector.tensor_copy)
+            if c == 2 and g + 1 < GROUPS:
+                mean_sq = add_halves(add_squares(g + 1))
             if 0 <= s - 1 < ALL_RUNS:
-                grouped_of[s - 1] = regroup(banks_of[s - 1], s % 3 == 1 and s + SQUARES_AHEAD < ALL_RUNS)
-            late = s - LAG
-            if 0 <= late < ALL_RUNS:
-                m, r = divmod(late, RUNS)
-                if r == 0:
-                    acc_of[m] = acc_pool.tile([P, N_OUT], F32, name="acc")
-                codes, plane = quantise(grouped_of[late])
-                project(r, codes, plane, acc_of[m])
-                if r == RUNS - 1:
-                    qkv_of[m] = collect(acc_of[m])
-            if next_tile_is_near:
-                invert((s + 1) // RUNS, rms)
-            done = s - LAG - 1
-            if done >= 0 and done % RUNS == RUNS - 1:
-                rope_and_store(done // RUNS, qkv_of[done // RUNS])
+                quantises = RUNS <= s - 2 and (s - 2) // RUNS % 2 == 1
+                regroup(s - 1, banks_of[s - 1], 1 if (squares_left and not quantises and s % 2 == 1) or s == ALL_RUNS else 0)
+            if c == 2 and g + 1 < GROUPS:
+                rms = root(mean_sq)
+            if c == 3 and g + 1 < GROUPS:
+                invert(g + 1, rms)
+            if s == RUNS:
+                fill_rope_tables()
+            for m in to_rope:
+                rope_and_store(m)
+            to_rope = []
+            late = s - 1 if s > ALL_RUNS - RUNS else s - 2
+            if 0 <= late < ALL_RUNS and late // RUNS % 2 == 1:
+                quantise(late // (2 * RUNS), late % RUNS)
+            now = PASSES_A_STEP if s < ALL_RUNS - 1 else len(waiting)
+            for m, k_pass, first, last, codes, plane in waiting[:now]:
+                project(m, k_pass, first, last, codes, plane)
+                if last:
+                    to_rope.append(m)
+            waiting[:] = waiting[now:]
+        for m in to_rope:
+            rope_and_store(m)

@@ -25,8 +25,10 @@ K_PASS = 4 * P
 PASSES = DIM // K_PASS
 RUN_K = 4 * K_PASS
 RUN = RUN_K // K_PASS
+BANK_K = 2 * K_PASS
 RUNS = HALF // RUN_K
 ALL_RUNS = GROUPS * RUNS
+PLANE_COLUMNS = 8
 CHUNKS = HALF // K_PASS
 N_Q, N_K, N_V = 256, 128, 128
 N_OUT = N_Q + N_K + N_V
@@ -34,7 +36,8 @@ N_ROPE = N_Q + N_K
 HEADS = N_ROPE // 32
 PAIRS = 16
 SQUARES_AHEAD = RUNS + 2
-PASSES_A_STEP = 5
+PASSES_A_STEP = 6
+WEIGHT_LAG = 4
 
 FLOPS = 2 * TOKENS * DIM * N_OUT
 
@@ -63,7 +66,7 @@ def tile_transformerblock_pa_k_kernel(
         x_pool = stack.enter_context(tc.tile_pool(name="x_pool", bufs=12))
         h_pool = stack.enter_context(tc.tile_pool(name="h_pool", bufs=3))
         grouped_pool = stack.enter_context(tc.tile_pool(name="grouped_pool", bufs=RUNS + 1))
-        code_pool = stack.enter_context(tc.tile_pool(name="code_pool", bufs=4))
+        code_pool = stack.enter_context(tc.tile_pool(name="code_pool", bufs=6))
         scrap_pool = stack.enter_context(tc.tile_pool(name="scrap_pool", bufs=1))
         small_pool = stack.enter_context(tc.tile_pool(name="small_pool", bufs=2))
         out_pool = stack.enter_context(tc.tile_pool(name="out_pool", bufs=2))
@@ -91,22 +94,38 @@ def tile_transformerblock_pa_k_kernel(
         sin_bf16 = keep.tile([P, TOKEN_TILES, PAIRS], BF16)
         nc.sync.dma_start(out=cos_bf16[:], in_=freqs_cos.rearrange("(m p) j -> p m j", p=P))
         nc.sync.dma_start(out=sin_bf16[:], in_=freqs_sin.rearrange("(m p) j -> p m j", p=P))
-        for s in range(2 * RUNS, 3 * RUNS):
-            load_x(s)
+        load_x(2 * RUNS)
+        load_x(2 * RUNS + 1)
+
+        w_planes = keep.tile([P, PLANE_COLUMNS, N_OUT], U8, align_bytes=64)
+        nc.vector.memset(w_planes[:].rearrange("p a n -> p (a n)").bitcast(I32), 0)
+        for j in range(PASSES // PLANE_COLUMNS):
+            for quadrant in range(4):
+                first_row = 32 * quadrant + 4 * j
+                for unused_words, scales, first, width in weights:
+                    nc.sync.dma_start(
+                        out=w_planes[first_row : first_row + 4, :, first : first + width].bitcast(I32),
+                        in_=scales[PLANE_COLUMNS * j : PLANE_COLUMNS * (j + 1), 4 * quadrant : 4 * quadrant + 4, :]
+                        .rearrange("a q n -> q a n")
+                        .bitcast(I32),
+                    )
 
         w_words = keep.tile([P, PASSES, N_OUT], I32, align_bytes=64)
 
-        def load_weights(first_pass):
-            passes = slice(first_pass, first_pass + RUN)
-            for words, unused_scales, first, width in weights:
+        def load_weights(block):
+            c, h, part = block // 4, block // 2 % 2, block % 2
+            passes = slice(CHUNKS * h + RUN * c, CHUNKS * h + RUN * (c + 1))
+            for words, unused_scales, first, width in weights[:1] if part == 0 else weights[1:]:
                 nc.sync.dma_start(
                     out=w_words[:, passes, first : first + width],
                     in_=words[passes].rearrange("g p n t -> p g (n t)").bitcast(I32),
                 )
 
-        for c in range(RUNS):
-            for h in range(2):
-                load_weights(CHUNKS * h + RUN * c)
+        load_weights(0)
+        load_weights(1)
+        load_x(2 * RUNS + 2)
+        load_weights(2)
+        load_x(2 * RUNS + 3)
 
         eps_col = keep.tile([P, 1], F32)
         nc.vector.memset(eps_col[:], EPS)
@@ -119,15 +138,6 @@ def tile_transformerblock_pa_k_kernel(
 
         ident = keep.tile([P, P], F32)
         make_identity(nc, ident[:])
-
-        w_planes = keep.tile([P, PASSES, N_OUT], U8, align_bytes=64)
-        nc.gpsimd.memset(w_planes[:].rearrange("p g n -> p (g n)").bitcast(I32), 0)
-        for quadrant in range(4):
-            for unused_words, scales, first, width in weights:
-                nc.gpsimd.dma_start(
-                    out=w_planes[32 * quadrant : 32 * quadrant + 4, :, first : first + width].bitcast(F32),
-                    in_=scales[:, 4 * quadrant : 4 * quadrant + 4, :].rearrange("g q n -> q g n").bitcast(F32),
-                )
 
         select = keep.tile([P, CHUNKS, GROUP, 2], BF16)
         nc.vector.tensor_copy(
@@ -209,23 +219,24 @@ def tile_transformerblock_pa_k_kernel(
         def invert(g, rms):
             nc.vector.reciprocal(out=rstd[:, g : g + 1], in_=rms[:])
 
-        def normalise(s):
+        def normalise(s, banks):
             g, c = divmod(s, RUNS)
             h = h_pool.tile([P, RUN_K], BF16, tag="h")
+            columns = slice(BANK_K * banks[0], BANK_K * (banks[-1] + 1))
             nc.vector.scalar_tensor_tensor(
-                out=h[:],
-                in0=x_pieces[s][:],
+                out=h[:, columns],
+                in0=x_pieces[s][:, columns],
                 scalar=rstd[:, g : g + 1],
-                in1=gain[:, RUN_K * c : RUN_K * (c + 1)],
+                in1=gain[:, RUN_K * c + columns.start : RUN_K * c + columns.stop],
                 op0=ALU.mult,
                 op1=ALU.mult,
             )
             return h
 
-        def transpose(h):
+        def transpose(h, banks):
             h_words = h[:].bitcast(F32)
-            banks = []
-            for b in range(RUN // 2):
+            transposed = []
+            for b in banks:
                 bank = bank_pool.tile([P, 2, 2, P], F32, tag="bank")
                 for u in range(2):
                     for i in range(2):
@@ -235,15 +246,15 @@ def tile_transformerblock_pa_k_kernel(
                             in_=h_words[:, first + u : first + K_PASS // 2 : 2],
                             identity=permute[:].rearrange("k h t -> k (h t)"),
                         )
-                banks.append(bank)
-            return banks
+                transposed.append(bank)
+            return transposed
 
         grouped_tiles = {}
 
-        def regroup(s, banks, vector_share):
+        def regroup(s, banks, transposed, vector_share):
             g, c = divmod(s, RUNS)
             m, part = divmod(g, 2)
-            if part == 0:
+            if (m, c) not in grouped_tiles:
                 grouped_tiles[m, c] = grouped_pool.tile([P, 2 * RUN, P, 4], BF16, align_bytes=64, name="grouped")
             grouped_words = (
                 grouped_tiles[m, c][:]
@@ -251,28 +262,32 @@ def tile_transformerblock_pa_k_kernel(
                 .bitcast(F32)
                 .rearrange("p (i j u) -> p i j u", i=2 * RUN, u=2)
             )
-            for b in range(RUN // 2):
-                copy_out = nc.vector.tensor_copy if b >= RUN // 2 - vector_share else nc.scalar.copy
+            for n, b in enumerate(banks):
+                copy_out = nc.vector.tensor_copy if n >= len(banks) - vector_share else nc.scalar.copy
                 copy_out(
                     out=grouped_words[:, 4 * b : 4 * b + 4, GROUP * part : GROUP * (part + 1)],
-                    in_=banks[b][:].rearrange("p u i (h j) -> p (i h) j u", h=2),
+                    in_=transposed[n][:].rearrange("p u i (h j) -> p (i h) j u", h=2),
                 )
 
         waiting = []
 
-        def quantise(m, c):
-            grouped = grouped_tiles[m, c]
-            codes = code_pool.tile([P, 2 * RUN * P], U32, align_bytes=64)
-            plane = code_pool.tile([P, 2 * RUN * P], U8, align_bytes=64)
+        def quantise(s, banks):
+            g, c = divmod(s, RUNS)
+            m = g // 2
+            first, last = 4 * banks[0], 4 * (banks[-1] + 1)
+            codes = code_pool.tile([P, 2 * RUN, P], U32, align_bytes=64)
+            plane = code_pool.tile([P, 2 * RUN, P], U8, align_bytes=64)
             nc.vector.quantize_mx(
-                out=codes[:].bitcast(FP8X4), scales=plane[:], in_=grouped[:].rearrange("p i j t -> p (i j t)")
+                out=codes[:, first:last].rearrange("p i j -> p (i j)").bitcast(FP8X4),
+                scales=plane[:, first:last].rearrange("p i j -> p (i j)"),
+                in_=grouped_tiles[m, c][:, first:last].rearrange("p i j t -> p (i j t)"),
             )
-            for i in range(2 * RUN):
-                tokens = slice(P * i, P * (i + 1))
+            for i in range(first, last):
                 k_pass = CHUNKS * (i % 2) + RUN * c + i // 2
-                waiting.append((m, k_pass, c == 0 and i == 0, c == RUNS - 1 and i == 2 * RUN - 1, codes[:, tokens], plane[:, tokens]))
+                waiting.append((4 * (c if m == 0 else RUNS - 1) + WEIGHT_LAG, m, k_pass, c == 0 and i == 0, c == RUNS - 1 and i == 2 * RUN - 1, codes[:, i], plane[:, i]))
 
         acc_of = {}
+        to_rope = []
 
         def project(m, k_pass, first, last, codes, plane):
             if first:
@@ -282,10 +297,12 @@ def tile_transformerblock_pa_k_kernel(
                 lhsT=codes.bitcast(FP8X4),
                 lhsT_scale=plane,
                 rhs=w_words[:, k_pass, :].bitcast(FP8X4),
-                rhs_scale=w_planes[:, k_pass, :],
+                rhs_scale=w_planes[4 * (k_pass // PLANE_COLUMNS) : P, k_pass % PLANE_COLUMNS, :],
                 start=first,
                 stop=last,
             )
+            if last:
+                to_rope.append(m)
 
         cos_pair = keep.tile([P, TOKEN_TILES, PAIRS, 2], F32)
         sin_plus = keep.tile([P, TOKEN_TILES, PAIRS], F32)
@@ -302,7 +319,7 @@ def tile_transformerblock_pa_k_kernel(
             rows = slice(P * m, P * (m + 1))
             acc = acc_of[m]
             value = out_pool.tile([P, N_V], F32)
-            nc.scalar.copy(out=value[:], in_=acc[:, N_ROPE:N_OUT])
+            nc.vector.tensor_copy(out=value[:], in_=acc[:, N_ROPE:N_OUT])
             nc.sync.dma_start(out=out_2[rows].rearrange("t h d -> t (h d)"), in_=value[:])
             pairs = acc[:, 0:N_ROPE].rearrange("p (h j e) -> p h j e", h=HEADS, e=2)
             own = rope_pool.tile([P, HEADS, PAIRS, 2], F32)
@@ -354,18 +371,27 @@ def tile_transformerblock_pa_k_kernel(
         for s in range(RUNS, SQUARES_AHEAD):
             square_on_scalar(s)
 
-        banks_of = {}
-        to_rope = []
-        for s in range(ALL_RUNS + 1):
+        steps = [(s, (0, 1)) for s in range(ALL_RUNS - 0)]
+        for s in range(ALL_RUNS - 0, ALL_RUNS):
+            steps += [(s, (0,)), (s, (1,))]
+        transposed_of = {}
+        for k in range(len(steps) + 1):
+            s, banks = steps[k] if k < len(steps) else (ALL_RUNS, ())
             g, c = divmod(s, RUNS)
+            opens = banks and banks[0] == 0
             squares_left = s + SQUARES_AHEAD < ALL_RUNS
-            if s < ALL_RUNS:
-                h = normalise(s)
-                if s + 3 * RUNS < ALL_RUNS:
+
+            if c == 3 and g + 1 < GROUPS:
+                rms = root(mean_sq)
+            if banks:
+                h = normalise(s, banks)
+                if opens and s + 3 * RUNS < ALL_RUNS:
                     load_x(s + 3 * RUNS)
+                if s + 3 < 4 * RUNS:
+                    load_weights(s + 3)
                 if squares_left:
                     square_on_scalar(s + SQUARES_AHEAD)
-                banks_of[s] = transpose(h)
+                transposed_of[k] = transpose(h, banks)
             if s == 0:
                 keep_gain(5, spreads[5], nc.vector.tensor_copy)
             if s == 1:
@@ -373,26 +399,24 @@ def tile_transformerblock_pa_k_kernel(
                 keep_gain(7, spreads[7], nc.vector.tensor_copy)
             if c == 2 and g + 1 < GROUPS:
                 mean_sq = add_halves(add_squares(g + 1))
-            if 0 <= s - 1 < ALL_RUNS:
+            if k > 0:
+                before, banks_before = steps[k - 1]
                 quantises = RUNS <= s - 2 and (s - 2) // RUNS % 2 == 1
-                regroup(s - 1, banks_of[s - 1], 1 if (squares_left and not quantises and s % 2 == 1) or s == ALL_RUNS else 0)
-            if c == 2 and g + 1 < GROUPS:
-                rms = root(mean_sq)
+                regroup(before, banks_before, transposed_of[k - 1], 1 if (squares_left and not quantises) or s == ALL_RUNS else 0)
             if c == 3 and g + 1 < GROUPS:
                 invert(g + 1, rms)
             if s == RUNS:
                 fill_rope_tables()
             for m in to_rope:
                 rope_and_store(m)
-            to_rope = []
-            late = s - 1 if s > ALL_RUNS - RUNS else s - 2
-            if 0 <= late < ALL_RUNS and late // RUNS % 2 == 1:
-                quantise(late // (2 * RUNS), late % RUNS)
+            to_rope.clear()
+            late = k - 1 if s > ALL_RUNS - RUNS else k - 2
+            if late >= 0 and steps[late][0] // RUNS % 2 == 1:
+                quantise(*steps[late])
             now = PASSES_A_STEP if s < ALL_RUNS - 1 else len(waiting)
-            for m, k_pass, first, last, codes, plane in waiting[:now]:
-                project(m, k_pass, first, last, codes, plane)
-                if last:
-                    to_rope.append(m)
-            waiting[:] = waiting[now:]
+            ready = [operands for operands in waiting[:now] if operands[0] <= s]
+            for operands in ready:
+                project(*operands[1:])
+            waiting[:] = waiting[len(ready) :]
         for m in to_rope:
             rope_and_store(m)

@@ -28,7 +28,7 @@ RUN = RUN_K // K_PASS
 BANK_K = 2 * K_PASS
 RUNS = HALF // RUN_K
 ALL_RUNS = GROUPS * RUNS
-PLANE_COLUMNS = 8
+PLANE_COLUMNS = 16
 CHUNKS = HALF // K_PASS
 N_Q, N_K, N_V = 256, 128, 128
 N_OUT = N_Q + N_K + N_V
@@ -66,7 +66,7 @@ def tile_transformerblock_pa_k_kernel(
         x_pool = stack.enter_context(tc.tile_pool(name="x_pool", bufs=12))
         h_pool = stack.enter_context(tc.tile_pool(name="h_pool", bufs=3))
         grouped_pool = stack.enter_context(tc.tile_pool(name="grouped_pool", bufs=RUNS + 1))
-        code_pool = stack.enter_context(tc.tile_pool(name="code_pool", bufs=6))
+        code_pool = stack.enter_context(tc.tile_pool(name="code_pool", bufs=5))
         scrap_pool = stack.enter_context(tc.tile_pool(name="scrap_pool", bufs=1))
         small_pool = stack.enter_context(tc.tile_pool(name="small_pool", bufs=2))
         out_pool = stack.enter_context(tc.tile_pool(name="out_pool", bufs=2))
@@ -96,36 +96,6 @@ def tile_transformerblock_pa_k_kernel(
         nc.sync.dma_start(out=sin_bf16[:], in_=freqs_sin.rearrange("(m p) j -> p m j", p=P))
         load_x(2 * RUNS)
         load_x(2 * RUNS + 1)
-
-        w_planes = keep.tile([P, PLANE_COLUMNS, N_OUT], U8, align_bytes=64)
-        nc.vector.memset(w_planes[:].rearrange("p a n -> p (a n)").bitcast(I32), 0)
-        for j in range(PASSES // PLANE_COLUMNS):
-            for quadrant in range(4):
-                first_row = 32 * quadrant + 4 * j
-                for unused_words, scales, first, width in weights:
-                    nc.sync.dma_start(
-                        out=w_planes[first_row : first_row + 4, :, first : first + width].bitcast(I32),
-                        in_=scales[PLANE_COLUMNS * j : PLANE_COLUMNS * (j + 1), 4 * quadrant : 4 * quadrant + 4, :]
-                        .rearrange("a q n -> q a n")
-                        .bitcast(I32),
-                    )
-
-        w_words = keep.tile([P, PASSES, N_OUT], I32, align_bytes=64)
-
-        def load_weights(block):
-            c, h, part = block // 4, block // 2 % 2, block % 2
-            passes = slice(CHUNKS * h + RUN * c, CHUNKS * h + RUN * (c + 1))
-            for words, unused_scales, first, width in weights[:1] if part == 0 else weights[1:]:
-                nc.sync.dma_start(
-                    out=w_words[:, passes, first : first + width],
-                    in_=words[passes].rearrange("g p n t -> p g (n t)").bitcast(I32),
-                )
-
-        load_weights(0)
-        load_weights(1)
-        load_x(2 * RUNS + 2)
-        load_weights(2)
-        load_x(2 * RUNS + 3)
 
         eps_col = keep.tile([P, 1], F32)
         nc.vector.memset(eps_col[:], EPS)
@@ -157,6 +127,40 @@ def tile_transformerblock_pa_k_kernel(
             in1=by_half[:, 1].unsqueeze(2).to_broadcast([P, GROUP, 2]),
             op=ALU.add,
         )
+        w_planes = keep.tile([P, PLANE_COLUMNS, N_OUT], U8, align_bytes=64)
+        nc.vector.memset(w_planes[:].rearrange("p a n -> p (a n)").bitcast(I32), 0)
+
+        def load_scales(j):
+            for quadrant in range(4):
+                first_row = 32 * quadrant + 4 * j
+                for unused_words, scales, first, width in weights:
+                    nc.sync.dma_start(
+                        out=w_planes[first_row : first_row + 4, :, first : first + width].bitcast(I32),
+                        in_=scales[PLANE_COLUMNS * j : PLANE_COLUMNS * (j + 1), 4 * quadrant : 4 * quadrant + 4, :]
+                        .rearrange("a q n -> q a n")
+                        .bitcast(I32),
+                    )
+
+        w_words = keep.tile([P, PASSES, N_OUT], I32, align_bytes=64)
+
+        def load_weights(block):
+            c, h, part = block // 4, block // 2 % 2, block % 2
+            passes = slice(CHUNKS * h + RUN * c, CHUNKS * h + RUN * (c + 1))
+            for words, unused_scales, first, width in weights[:1] if part == 0 else weights[1:]:
+                nc.sync.dma_start(
+                    out=w_words[:, passes, first : first + width],
+                    in_=words[passes].rearrange("g p n t -> p g (n t)").bitcast(I32),
+                )
+
+        for j in range(PASSES // PLANE_COLUMNS):
+            load_scales(j)
+
+        load_weights(0)
+        load_weights(1)
+        load_x(2 * RUNS + 2)
+        load_weights(2)
+        load_x(2 * RUNS + 3)
+
         gain = keep.tile([P, HALF], BF16)
 
         def spread_gain(pair):

@@ -36,7 +36,7 @@ N_ROPE = N_Q + N_K
 HEADS = N_ROPE // 32
 PAIRS = 16
 SQUARES_AHEAD = RUNS + 2
-PASSES_A_STEP = 6
+PASSES_A_STEP = 7
 WEIGHT_LAG = 4
 
 FLOPS = 2 * TOKENS * DIM * N_OUT
@@ -225,29 +225,33 @@ def tile_transformerblock_pa_k_kernel(
 
         def normalise(s, banks):
             g, c = divmod(s, RUNS)
-            h = h_pool.tile([P, RUN_K], BF16, tag="h")
-            columns = slice(BANK_K * banks[0], BANK_K * (banks[-1] + 1))
-            nc.vector.scalar_tensor_tensor(
-                out=h[:, columns],
-                in0=x_pieces[s][:, columns],
-                scalar=rstd[:, g : g + 1],
-                in1=gain[:, RUN_K * c + columns.start : RUN_K * c + columns.stop],
-                op0=ALU.mult,
-                op1=ALU.mult,
-            )
+            h = h_pool.tile([P, 2, RUN, P, 2], BF16, tag="h")
+            first, last = BANK_K * banks[0], BANK_K * (banks[-1] + 1)
+            chunks = slice(2 * banks[0], 2 * (banks[-1] + 1))
+            x_words = x_pieces[s][:, first:last].rearrange("p (w u e) -> p u w e", u=2, e=2)
+            gain_words = gain[:, RUN_K * c + first : RUN_K * c + last].rearrange("p (w u e) -> p u w e", u=2, e=2)
+            for u in range(2):
+                nc.vector.scalar_tensor_tensor(
+                    out=h[:, u, chunks].rearrange("p i w e -> p (i w) e"),
+                    in0=x_words[:, u],
+                    scalar=rstd[:, g : g + 1],
+                    in1=gain_words[:, u],
+                    op0=ALU.mult,
+                    op1=ALU.mult,
+                )
             return h
 
         def transpose(h, banks):
-            h_words = h[:].bitcast(F32)
+            h_words = h[:].rearrange("p u i w e -> p (u i w e)").bitcast(F32)
             transposed = []
             for b in banks:
                 bank = bank_pool.tile([P, 2, 2, P], F32, tag="bank")
                 for u in range(2):
                     for i in range(2):
-                        first = (K_PASS // 2) * (2 * b + i)
+                        first = P * (RUN * u + 2 * b + i)
                         nc.tensor.transpose(
                             out=bank[:, u, i, :],
-                            in_=h_words[:, first + u : first + K_PASS // 2 : 2],
+                            in_=h_words[:, first : first + P],
                             identity=permute[:].rearrange("k h t -> k (h t)"),
                         )
                 transposed.append(bank)
@@ -406,7 +410,7 @@ def tile_transformerblock_pa_k_kernel(
             if k > 0:
                 before, banks_before = steps[k - 1]
                 quantises = RUNS <= s - 2 and (s - 2) // RUNS % 2 == 1
-                regroup(before, banks_before, transposed_of[k - 1], 1 if (squares_left and not quantises) or s == ALL_RUNS else 0)
+                regroup(before, banks_before, transposed_of[k - 1], 1 if (squares_left and (s < 6 or not quantises and s % 2 == 1)) or s == ALL_RUNS else 0)
             if c == 3 and g + 1 < GROUPS:
                 invert(g + 1, rms)
             if s == RUNS:
@@ -417,7 +421,7 @@ def tile_transformerblock_pa_k_kernel(
             late = k - 1 if s > ALL_RUNS - RUNS else k - 2
             if late >= 0 and steps[late][0] // RUNS % 2 == 1:
                 quantise(*steps[late])
-            now = PASSES_A_STEP if s < ALL_RUNS - 1 else len(waiting)
+            now = PASSES_A_STEP if s < ALL_RUNS - 3 else len(waiting)
             ready = [operands for operands in waiting[:now] if operands[0] <= s]
             for operands in ready:
                 project(*operands[1:])

@@ -82,13 +82,20 @@ def tile_transformerblock_pa_k_kernel(
         x_halves = x.rearrange("t (h k) -> (t h) k", h=2)
         x_pieces = {}
 
-        def load_x(s):
+        def load_x(s, half=None):
             g, c = divmod(s, RUNS)
-            piece = x_pool.tile([P, RUN_K], BF16)
-            nc.sync.dma_start(out=piece[:], in_=x_halves[P * g : P * (g + 1), RUN_K * c : RUN_K * (c + 1)])
-            x_pieces[s] = piece
+            if s not in x_pieces:
+                x_pieces[s] = x_pool.tile([P, RUN_K], BF16, name="piece")
+            first, last = (0, RUN_K) if half is None else (BANK_K * half, BANK_K * (half + 1))
+            nc.sync.dma_start(
+                out=x_pieces[s][:, first:last], in_=x_halves[P * g : P * (g + 1), RUN_K * c + first : RUN_K * c + last]
+            )
 
-        for s in range(2 * RUNS):
+        for s in range(0, RUNS, 2):
+            for half in range(2):
+                for piece in (s, s + 1):
+                    load_x(piece, half)
+        for s in range(RUNS, 2 * RUNS):
             load_x(s)
         cos_bf16 = keep.tile([P, TOKEN_TILES, PAIRS], BF16)
         sin_bf16 = keep.tile([P, TOKEN_TILES, PAIRS], BF16)
@@ -96,6 +103,7 @@ def tile_transformerblock_pa_k_kernel(
         nc.sync.dma_start(out=sin_bf16[:], in_=freqs_sin.rearrange("(m p) j -> p m j", p=P))
         load_x(2 * RUNS)
         load_x(2 * RUNS + 1)
+        load_x(2 * RUNS + 2)
 
         eps_col = keep.tile([P, 1], F32)
         nc.vector.memset(eps_col[:], EPS)
@@ -157,9 +165,8 @@ def tile_transformerblock_pa_k_kernel(
 
         load_weights(0)
         load_weights(1)
-        load_x(2 * RUNS + 2)
-        load_weights(2)
         load_x(2 * RUNS + 3)
+        load_weights(2)
 
         gain = keep.tile([P, HALF], BF16)
 
@@ -179,28 +186,32 @@ def tile_transformerblock_pa_k_kernel(
         def keep_gain(pair, spread, copy_out):
             copy_out(out=gain[:, 2 * K_PASS * pair : 2 * K_PASS * (pair + 1)], in_=spread[:])
 
-        def square_on_scalar(s):
+        def square_on_scalar(s, half=None):
             g, c = divmod(s, RUNS)
+            columns = slice(0, RUN_K) if half is None else slice(BANK_K * half, BANK_K * (half + 1))
+            place = c if half is None else c + half
             scrap = scrap_pool.tile([P, RUN_K], BF16)
             nc.scalar.activation(
-                out=scrap[:],
-                in_=x_pieces[s][:],
+                out=scrap[:, columns],
+                in_=x_pieces[s][:, columns],
                 func=ACT.Square,
                 scale=1.0 / 128.0,
-                accum_out=sums[:, g, c : c + 1],
+                accum_out=sums[:, g, place : place + 1],
             )
 
-        def square_on_vector(s):
+        def square_on_vector(s, half):
             g, c = divmod(s, RUNS)
+            columns = slice(BANK_K * half, BANK_K * (half + 1))
+            place = RUNS + c - 1 + half
             scrap = h_pool.tile([P, RUN_K], BF16, tag="h")
             nc.vector.scalar_tensor_tensor(
-                out=scrap[:],
-                in0=x_pieces[s][:],
+                out=scrap[:, columns],
+                in0=x_pieces[s][:, columns],
                 scalar=1.0 / DIM,
-                in1=x_pieces[s][:],
+                in1=x_pieces[s][:, columns],
                 op0=ALU.mult,
                 op1=ALU.mult,
-                accum_out=sums[:, g, RUNS + c : RUNS + c + 1],
+                accum_out=sums[:, g, place : place + 1],
             )
 
         def add_squares(g):
@@ -225,33 +236,29 @@ def tile_transformerblock_pa_k_kernel(
 
         def normalise(s, banks):
             g, c = divmod(s, RUNS)
-            h = h_pool.tile([P, 2, RUN, P, 2], BF16, tag="h")
-            first, last = BANK_K * banks[0], BANK_K * (banks[-1] + 1)
-            chunks = slice(2 * banks[0], 2 * (banks[-1] + 1))
-            x_words = x_pieces[s][:, first:last].rearrange("p (w u e) -> p u w e", u=2, e=2)
-            gain_words = gain[:, RUN_K * c + first : RUN_K * c + last].rearrange("p (w u e) -> p u w e", u=2, e=2)
-            for u in range(2):
-                nc.vector.scalar_tensor_tensor(
-                    out=h[:, u, chunks].rearrange("p i w e -> p (i w) e"),
-                    in0=x_words[:, u],
-                    scalar=rstd[:, g : g + 1],
-                    in1=gain_words[:, u],
-                    op0=ALU.mult,
-                    op1=ALU.mult,
-                )
+            h = h_pool.tile([P, RUN_K], BF16, tag="h")
+            columns = slice(BANK_K * banks[0], BANK_K * (banks[-1] + 1))
+            nc.vector.scalar_tensor_tensor(
+                out=h[:, columns],
+                in0=x_pieces[s][:, columns],
+                scalar=rstd[:, g : g + 1],
+                in1=gain[:, RUN_K * c + columns.start : RUN_K * c + columns.stop],
+                op0=ALU.mult,
+                op1=ALU.mult,
+            )
             return h
 
         def transpose(h, banks):
-            h_words = h[:].rearrange("p u i w e -> p (u i w e)").bitcast(F32)
+            h_words = h[:].bitcast(F32)
             transposed = []
             for b in banks:
                 bank = bank_pool.tile([P, 2, 2, P], F32, tag="bank")
                 for u in range(2):
                     for i in range(2):
-                        first = P * (RUN * u + 2 * b + i)
+                        first = (K_PASS // 2) * (2 * b + i)
                         nc.tensor.transpose(
                             out=bank[:, u, i, :],
-                            in_=h_words[:, first : first + P],
+                            in_=h_words[:, first + u : first + K_PASS // 2 : 2],
                             identity=permute[:].rearrange("k h t -> k (h t)"),
                         )
                 transposed.append(bank)
@@ -290,27 +297,34 @@ def tile_transformerblock_pa_k_kernel(
                 scales=plane[:, first:last].rearrange("p i j -> p (i j)"),
                 in_=grouped_tiles[m, c][:, first:last].rearrange("p i j t -> p (i j t)"),
             )
-            for i in range(first, last):
-                k_pass = CHUNKS * (i % 2) + RUN * c + i // 2
-                waiting.append((4 * (c if m == 0 else RUNS - 1) + WEIGHT_LAG, m, k_pass, c == 0 and i == 0, c == RUNS - 1 and i == 2 * RUN - 1, codes[:, i], plane[:, i]))
+            parts = ((0, N_OUT),) if m < TOKEN_TILES - 1 else ((0, N_Q), (N_Q, N_OUT))
+            earliest = 4 * (c if m == 0 else RUNS - 1) + WEIGHT_LAG
+            for part in range(len(parts)):
+                for i in range(first, last):
+                    waiting.append((earliest, s, part, parts[part], i, codes[:, i], plane[:, i]))
 
         acc_of = {}
         to_rope = []
 
-        def project(m, k_pass, first, last, codes, plane):
-            if first:
-                acc_of[m] = acc_pool.tile([P, N_OUT], F32, name="acc")
+        def project(s, part, columns, i, codes, plane):
+            g, c = divmod(s, RUNS)
+            m = g // 2
+            k_pass = CHUNKS * (i % 2) + RUN * c + i // 2
+            first, last = columns
+            if (m, part) not in acc_of:
+                acc_of[m, part] = acc_pool.tile([P, N_OUT], F32, name="acc")
+            ends = c == RUNS - 1 and i == 2 * RUN - 1
             nc.tensor.matmul_mx(
-                out=acc_of[m][:],
+                out=acc_of[m, part][:, 0 : last - first],
                 lhsT=codes.bitcast(FP8X4),
                 lhsT_scale=plane,
-                rhs=w_words[:, k_pass, :].bitcast(FP8X4),
-                rhs_scale=w_planes[4 * (k_pass // PLANE_COLUMNS) : P, k_pass % PLANE_COLUMNS, :],
-                start=first,
-                stop=last,
+                rhs=w_words[:, k_pass, first:last].bitcast(FP8X4),
+                rhs_scale=w_planes[4 * (k_pass // PLANE_COLUMNS) : P, k_pass % PLANE_COLUMNS, first:last],
+                start=c == 0 and i == 0,
+                stop=ends,
             )
-            if last:
-                to_rope.append(m)
+            if ends:
+                to_rope.append((m, part))
 
         cos_pair = keep.tile([P, TOKEN_TILES, PAIRS, 2], F32)
         sin_plus = keep.tile([P, TOKEN_TILES, PAIRS], F32)
@@ -323,52 +337,70 @@ def tile_transformerblock_pa_k_kernel(
             nc.vector.tensor_copy(out=sin_plus[:], in_=sin_bf16[:])
             nc.vector.tensor_scalar_mul(out=sin_minus[:], in0=sin_bf16[:], scalar1=-1.0)
 
-        def rope_and_store(m):
-            rows = slice(P * m, P * (m + 1))
-            acc = acc_of[m]
-            value = out_pool.tile([P, N_V], F32)
-            nc.vector.tensor_copy(out=value[:], in_=acc[:, N_ROPE:N_OUT])
-            nc.sync.dma_start(out=out_2[rows].rearrange("t h d -> t (h d)"), in_=value[:])
-            pairs = acc[:, 0:N_ROPE].rearrange("p (h j e) -> p h j e", h=HEADS, e=2)
-            own = rope_pool.tile([P, HEADS, PAIRS, 2], F32)
-            nc.vector.tensor_tensor(
-                out=own[:],
-                in0=pairs,
-                in1=cos_pair[:, m].unsqueeze(1).to_broadcast([P, HEADS, PAIRS, 2]),
-                op=ALU.mult,
-            )
+        def rotate(m, bank, heads, stores):
+            pairs = bank[:, 0 : 2 * PAIRS * heads].rearrange("p (h j e) -> p h j e", h=heads, e=2)
             other = rope_pool.tile([P, 2, HEADS, PAIRS], F32)
             nc.vector.tensor_tensor(
-                out=other[:, 0],
+                out=other[:, 0, 0:heads],
                 in0=pairs[:, :, :, 1],
-                in1=sin_minus[:, m].unsqueeze(1).to_broadcast([P, HEADS, PAIRS]),
+                in1=sin_minus[:, m].unsqueeze(1).to_broadcast([P, heads, PAIRS]),
                 op=ALU.mult,
             )
             nc.vector.tensor_tensor(
-                out=other[:, 1],
+                out=other[:, 1, 0:heads],
                 in0=pairs[:, :, :, 0],
-                in1=sin_plus[:, m].unsqueeze(1).to_broadcast([P, HEADS, PAIRS]),
+                in1=sin_plus[:, m].unsqueeze(1).to_broadcast([P, heads, PAIRS]),
+                op=ALU.mult,
+            )
+            own = rope_pool.tile([P, HEADS, PAIRS, 2], F32)
+            nc.vector.tensor_tensor(
+                out=own[:, 0:heads],
+                in0=pairs,
+                in1=cos_pair[:, m].unsqueeze(1).to_broadcast([P, heads, PAIRS, 2]),
                 op=ALU.mult,
             )
             rotated = out_pool.tile([P, N_ROPE], F32)
             nc.vector.tensor_tensor(
-                out=rotated[:].rearrange("p (n e) -> p n e", e=2),
-                in0=own[:].rearrange("p h j e -> p (h j) e"),
-                in1=other[:].rearrange("p e h j -> p (h j) e"),
+                out=rotated[:, 0 : 2 * PAIRS * heads].rearrange("p (n e) -> p n e", e=2),
+                in0=own[:, 0:heads].rearrange("p h j e -> p (h j) e"),
+                in1=other[:, :, 0:heads].rearrange("p e h j -> p (h j) e"),
                 op=ALU.add,
             )
-            nc.sync.dma_start(out=out_0[rows].rearrange("t h d -> t (h d)"), in_=rotated[:, 0:N_Q])
-            nc.sync.dma_start(out=out_1[rows].rearrange("t h d -> t (h d)"), in_=rotated[:, N_Q:N_ROPE])
+            rows = slice(P * m, P * (m + 1))
+            first = 0
+            for out, width in stores:
+                nc.sync.dma_start(
+                    out=out[rows].rearrange("t h d -> t (h d)"), in_=rotated[:, first : first + width]
+                )
+                first += width
+
+        def keep_value(m, columns, copy_out):
+            value = out_pool.tile([P, N_V], F32)
+            copy_out(out=value[:], in_=columns)
+            nc.sync.dma_start(out=out_2[P * m : P * (m + 1)].rearrange("t h d -> t (h d)"), in_=value[:])
+
+        def finish(m, part):
+            bank = acc_of[m, part]
+            if m < TOKEN_TILES - 1:
+                keep_value(m, bank[:, N_ROPE:N_OUT], nc.vector.tensor_copy)
+                rotate(m, bank, HEADS, ((out_0, N_Q), (out_1, N_K)))
+            elif part == 0:
+                rotate(m, bank, N_Q // (2 * PAIRS), ((out_0, N_Q),))
+            else:
+                rotate(m, bank, N_K // (2 * PAIRS), ((out_1, N_K),))
+                keep_value(m, bank[:, N_K : N_K + N_V], nc.scalar.copy)
 
         spreads = []
         for pair in range(6):
             spreads.append(spread_gain(pair))
         keep_gain(0, spreads[0], nc.scalar.copy)
-        square_on_scalar(0)
-        square_on_vector(1)
-        square_on_scalar(2)
+        for half in range(2):
+            square_on_scalar(0, half)
+            square_on_vector(1, half)
         keep_gain(1, spreads[1], nc.vector.tensor_copy)
-        square_on_vector(3)
+        for half in range(2):
+            square_on_scalar(2, half)
+            square_on_vector(3, half)
         rms = root(add_halves(add_squares(0)))
         keep_gain(3, spreads[3], nc.vector.tensor_copy)
         keep_gain(4, spreads[4], nc.vector.tensor_copy)
@@ -415,8 +447,8 @@ def tile_transformerblock_pa_k_kernel(
                 invert(g + 1, rms)
             if s == RUNS:
                 fill_rope_tables()
-            for m in to_rope:
-                rope_and_store(m)
+            for m, part in to_rope:
+                finish(m, part)
             to_rope.clear()
             late = k - 1 if s > ALL_RUNS - RUNS else k - 2
             if late >= 0 and steps[late][0] // RUNS % 2 == 1:
@@ -426,5 +458,5 @@ def tile_transformerblock_pa_k_kernel(
             for operands in ready:
                 project(*operands[1:])
             waiting[:] = waiting[len(ready) :]
-        for m in to_rope:
-            rope_and_store(m)
+        for m, part in to_rope:
+            finish(m, part)

@@ -35,7 +35,7 @@ N_OUT = N_Q + N_K + N_V
 N_ROPE = N_Q + N_K
 HEADS = N_ROPE // 32
 PAIRS = 16
-SQUARES_AHEAD = RUNS + 2
+SQUARES_AHEAD = RUNS + 1
 PASSES_A_STEP = 7
 WEIGHT_LAG = 4
 
@@ -234,39 +234,37 @@ def tile_transformerblock_pa_k_kernel(
         def invert(g, rms):
             nc.vector.reciprocal(out=rstd[:, g : g + 1], in_=rms[:])
 
-        def normalise(s, banks):
+        def normalise(s):
             g, c = divmod(s, RUNS)
             h = h_pool.tile([P, RUN_K], BF16, tag="h")
-            columns = slice(BANK_K * banks[0], BANK_K * (banks[-1] + 1))
-            nc.vector.scalar_tensor_tensor(
-                out=h[:, columns],
-                in0=x_pieces[s][:, columns],
-                scalar=rstd[:, g : g + 1],
-                in1=gain[:, RUN_K * c + columns.start : RUN_K * c + columns.stop],
-                op0=ALU.mult,
-                op1=ALU.mult,
-            )
+            for b in range(RUN // 2):
+                columns = slice(BANK_K * b, BANK_K * (b + 1))
+                nc.vector.scalar_tensor_tensor(
+                    out=h[:, columns],
+                    in0=x_pieces[s][:, columns],
+                    scalar=rstd[:, g : g + 1],
+                    in1=gain[:, RUN_K * c + columns.start : RUN_K * c + columns.stop],
+                    op0=ALU.mult,
+                    op1=ALU.mult,
+                )
             return h
 
-        def transpose(h, banks):
+        def transpose(h, b):
             h_words = h[:].bitcast(F32)
-            transposed = []
-            for b in banks:
-                bank = bank_pool.tile([P, 2, 2, P], F32, tag="bank")
-                for u in range(2):
-                    for i in range(2):
-                        first = (K_PASS // 2) * (2 * b + i)
-                        nc.tensor.transpose(
-                            out=bank[:, u, i, :],
-                            in_=h_words[:, first + u : first + K_PASS // 2 : 2],
-                            identity=permute[:].rearrange("k h t -> k (h t)"),
-                        )
-                transposed.append(bank)
-            return transposed
+            bank = bank_pool.tile([P, 2, 2, P], F32, tag="bank")
+            for u in range(2):
+                for i in range(2):
+                    first = (K_PASS // 2) * (2 * b + i)
+                    nc.tensor.transpose(
+                        out=bank[:, u, i, :],
+                        in_=h_words[:, first + u : first + K_PASS // 2 : 2],
+                        identity=permute[:].rearrange("k h t -> k (h t)"),
+                    )
+            return bank
 
         grouped_tiles = {}
 
-        def regroup(s, banks, transposed, vector_share):
+        def regroup(s, banks, vector_share):
             g, c = divmod(s, RUNS)
             m, part = divmod(g, 2)
             if (m, c) not in grouped_tiles:
@@ -277,30 +275,29 @@ def tile_transformerblock_pa_k_kernel(
                 .bitcast(F32)
                 .rearrange("p (i j u) -> p i j u", i=2 * RUN, u=2)
             )
-            for n, b in enumerate(banks):
-                copy_out = nc.vector.tensor_copy if n >= len(banks) - vector_share else nc.scalar.copy
+            for b in range(RUN // 2):
+                copy_out = nc.vector.tensor_copy if b >= RUN // 2 - vector_share else nc.scalar.copy
                 copy_out(
                     out=grouped_words[:, 4 * b : 4 * b + 4, GROUP * part : GROUP * (part + 1)],
-                    in_=transposed[n][:].rearrange("p u i (h j) -> p (i h) j u", h=2),
+                    in_=banks[b][:].rearrange("p u i (h j) -> p (i h) j u", h=2),
                 )
 
         waiting = []
 
-        def quantise(s, banks):
+        def quantise(s):
             g, c = divmod(s, RUNS)
             m = g // 2
-            first, last = 4 * banks[0], 4 * (banks[-1] + 1)
             codes = code_pool.tile([P, 2 * RUN, P], U32, align_bytes=64)
             plane = code_pool.tile([P, 2 * RUN, P], U8, align_bytes=64)
             nc.vector.quantize_mx(
-                out=codes[:, first:last].rearrange("p i j -> p (i j)").bitcast(FP8X4),
-                scales=plane[:, first:last].rearrange("p i j -> p (i j)"),
-                in_=grouped_tiles[m, c][:, first:last].rearrange("p i j t -> p (i j t)"),
+                out=codes[:].rearrange("p i j -> p (i j)").bitcast(FP8X4),
+                scales=plane[:].rearrange("p i j -> p (i j)"),
+                in_=grouped_tiles[m, c][:].rearrange("p i j t -> p (i j t)"),
             )
             parts = ((0, N_OUT),) if m < TOKEN_TILES - 1 else ((0, N_Q), (N_Q, N_OUT))
             earliest = 4 * (c if m == 0 else RUNS - 1) + WEIGHT_LAG
             for part in range(len(parts)):
-                for i in range(first, last):
+                for i in range(2 * RUN):
                     waiting.append((earliest, s, part, parts[part], i, codes[:, i], plane[:, i]))
 
         acc_of = {}
@@ -390,6 +387,12 @@ def tile_transformerblock_pa_k_kernel(
                 rotate(m, bank, N_K // (2 * PAIRS), ((out_1, N_K),))
                 keep_value(m, bank[:, N_K : N_K + N_V], nc.scalar.copy)
 
+        def multiply(s, most):
+            ready = [operands for operands in waiting[:most] if operands[0] <= s]
+            for operands in ready:
+                project(*operands[1:])
+            waiting[:] = waiting[len(ready) :]
+
         spreads = []
         for pair in range(6):
             spreads.append(spread_gain(pair))
@@ -411,52 +414,43 @@ def tile_transformerblock_pa_k_kernel(
         for s in range(RUNS, SQUARES_AHEAD):
             square_on_scalar(s)
 
-        steps = [(s, (0, 1)) for s in range(ALL_RUNS - 0)]
-        for s in range(ALL_RUNS - 0, ALL_RUNS):
-            steps += [(s, (0,)), (s, (1,))]
         transposed_of = {}
-        for k in range(len(steps) + 1):
-            s, banks = steps[k] if k < len(steps) else (ALL_RUNS, ())
+        for s in range(ALL_RUNS + 1):
             g, c = divmod(s, RUNS)
-            opens = banks and banks[0] == 0
             squares_left = s + SQUARES_AHEAD < ALL_RUNS
-
             if c == 3 and g + 1 < GROUPS:
-                rms = root(mean_sq)
-            if banks:
-                h = normalise(s, banks)
-                if opens and s + 3 * RUNS < ALL_RUNS:
+                mean_sq = add_halves(add_squares(g + 1))
+                multiply(s, PASSES_A_STEP)
+            if s < ALL_RUNS:
+                h = normalise(s)
+                if s + 3 * RUNS < ALL_RUNS:
                     load_x(s + 3 * RUNS)
                 if s + 3 < 4 * RUNS:
                     load_weights(s + 3)
                 if squares_left:
                     square_on_scalar(s + SQUARES_AHEAD)
-                transposed_of[k] = transpose(h, banks)
+                transposed_of[s] = [transpose(h, 0), transpose(h, 1)]
             if s == 0:
                 keep_gain(5, spreads[5], nc.vector.tensor_copy)
             if s == 1:
                 keep_gain(6, spreads[6], nc.vector.tensor_copy)
                 keep_gain(7, spreads[7], nc.vector.tensor_copy)
-            if c == 2 and g + 1 < GROUPS:
-                mean_sq = add_halves(add_squares(g + 1))
-            if k > 0:
-                before, banks_before = steps[k - 1]
-                quantises = RUNS <= s - 2 and (s - 2) // RUNS % 2 == 1
-                regroup(before, banks_before, transposed_of[k - 1], 1 if (squares_left and (s < 6 or not quantises and s % 2 == 1)) or s == ALL_RUNS else 0)
             if c == 3 and g + 1 < GROUPS:
-                invert(g + 1, rms)
+                rms = root(mean_sq)
+            if s > 0:
+                quantises = RUNS <= s - 2 and (s - 2) // RUNS % 2 == 1
+                regroup(s - 1, transposed_of[s - 1], 1 if (squares_left and (s < 6 or not quantises and s % 2 == 1)) or s == ALL_RUNS else 0)
             if s == RUNS:
                 fill_rope_tables()
             for m, part in to_rope:
                 finish(m, part)
             to_rope.clear()
-            late = k - 1 if s > ALL_RUNS - RUNS else k - 2
-            if late >= 0 and steps[late][0] // RUNS % 2 == 1:
-                quantise(*steps[late])
-            now = PASSES_A_STEP if s < ALL_RUNS - 3 else len(waiting)
-            ready = [operands for operands in waiting[:now] if operands[0] <= s]
-            for operands in ready:
-                project(*operands[1:])
-            waiting[:] = waiting[len(ready) :]
+            late = s - 1 if s > ALL_RUNS - RUNS else s - 2
+            if late >= 0 and late // RUNS % 2 == 1:
+                quantise(late)
+            if c != 2 or s > ALL_RUNS - 3:
+                multiply(s, PASSES_A_STEP if s < ALL_RUNS - 3 else len(waiting))
+            if c == 3 and g + 1 < GROUPS:
+                invert(g + 1, rms)
         for m, part in to_rope:
             finish(m, part)

@@ -37,7 +37,7 @@ HEADS = N_ROPE // 32
 PAIRS = 16
 SQUARES_AHEAD = RUNS + 1
 PASSES_A_STEP = 7
-WEIGHT_LAG = 4
+WEIGHT_LAG = 6
 
 FLOPS = 2 * TOKENS * DIM * N_OUT
 
@@ -101,9 +101,6 @@ def tile_transformerblock_pa_k_kernel(
         sin_bf16 = keep.tile([P, TOKEN_TILES, PAIRS], BF16)
         nc.sync.dma_start(out=cos_bf16[:], in_=freqs_cos.rearrange("(m p) j -> p m j", p=P))
         nc.sync.dma_start(out=sin_bf16[:], in_=freqs_sin.rearrange("(m p) j -> p m j", p=P))
-        load_x(2 * RUNS)
-        load_x(2 * RUNS + 1)
-        load_x(2 * RUNS + 2)
 
         eps_col = keep.tile([P, 1], F32)
         nc.vector.memset(eps_col[:], EPS)
@@ -138,16 +135,16 @@ def tile_transformerblock_pa_k_kernel(
         w_planes = keep.tile([P, PLANE_COLUMNS, N_OUT], U8, align_bytes=64)
         nc.vector.memset(w_planes[:].rearrange("p a n -> p (a n)").bitcast(I32), 0)
 
-        def load_scales(j):
-            for quadrant in range(4):
-                first_row = 32 * quadrant + 4 * j
-                for unused_words, scales, first, width in weights:
-                    nc.sync.dma_start(
-                        out=w_planes[first_row : first_row + 4, :, first : first + width].bitcast(I32),
-                        in_=scales[PLANE_COLUMNS * j : PLANE_COLUMNS * (j + 1), 4 * quadrant : 4 * quadrant + 4, :]
-                        .rearrange("a q n -> q a n")
-                        .bitcast(I32),
-                    )
+        def load_scales(part):
+            j, quadrant = divmod(part, 4)
+            first_row = 32 * quadrant + 4 * j
+            for unused_words, scales, first, width in weights:
+                nc.sync.dma_start(
+                    out=w_planes[first_row : first_row + 4, :, first : first + width].bitcast(I32),
+                    in_=scales[PLANE_COLUMNS * j : PLANE_COLUMNS * (j + 1), 4 * quadrant : 4 * quadrant + 4, :]
+                    .rearrange("a q n -> q a n")
+                    .bitcast(I32),
+                )
 
         w_words = keep.tile([P, PASSES, N_OUT], I32, align_bytes=64)
 
@@ -160,13 +157,21 @@ def tile_transformerblock_pa_k_kernel(
                     in_=words[passes].rearrange("g p n t -> p g (n t)").bitcast(I32),
                 )
 
-        for j in range(PASSES // PLANE_COLUMNS):
-            load_scales(j)
-
+        load_x(2 * RUNS)
+        load_scales(0)
+        load_x(2 * RUNS + 1)
+        load_scales(1)
+        load_x(2 * RUNS + 2)
+        load_scales(2)
         load_weights(0)
+        load_scales(3)
+        load_scales(4)
         load_weights(1)
+        load_scales(5)
         load_x(2 * RUNS + 3)
+        load_scales(6)
         load_weights(2)
+        load_scales(7)
 
         gain = keep.tile([P, HALF], BF16)
 

@@ -37,7 +37,7 @@ HEADS = N_ROPE // 32
 PAIRS = 16
 SQUARES_AHEAD = RUNS + 1
 PASSES_A_STEP = 7
-WEIGHT_LAG = 6
+WEIGHT_LAG = 5
 
 FLOPS = 2 * TOKENS * DIM * N_OUT
 

@@ -241,28 +241,29 @@ def tile_transformerblock_pa_k_kernel(
 
         def normalise(s):
             g, c = divmod(s, RUNS)
-            h = h_pool.tile([P, RUN_K], BF16, tag="h")
-            for b in range(RUN // 2):
-                columns = slice(BANK_K * b, BANK_K * (b + 1))
+            h = h_pool.tile([P, 2, RUN_K // 4, 2], BF16, tag="h")
+            x_words = x_pieces[s][:].rearrange("p (w u e) -> p u w e", u=2, e=2)
+            gain_words = gain[:, RUN_K * c : RUN_K * (c + 1)].rearrange("p (w u e) -> p u w e", u=2, e=2)
+            for u in range(2):
                 nc.vector.scalar_tensor_tensor(
-                    out=h[:, columns],
-                    in0=x_pieces[s][:, columns],
+                    out=h[:, u],
+                    in0=x_words[:, u],
                     scalar=rstd[:, g : g + 1],
-                    in1=gain[:, RUN_K * c + columns.start : RUN_K * c + columns.stop],
+                    in1=gain_words[:, u],
                     op0=ALU.mult,
                     op1=ALU.mult,
                 )
             return h
 
         def transpose(h, b):
-            h_words = h[:].bitcast(F32)
+            h_words = h[:].rearrange("p u w e -> p (u w e)").bitcast(F32)
             bank = bank_pool.tile([P, 2, 2, P], F32, tag="bank")
             for u in range(2):
                 for i in range(2):
-                    first = (K_PASS // 2) * (2 * b + i)
+                    first = P * (RUN * u + 2 * b + i)
                     nc.tensor.transpose(
                         out=bank[:, u, i, :],
-                        in_=h_words[:, first + u : first + K_PASS // 2 : 2],
+                        in_=h_words[:, first : first + P],
                         identity=permute[:].rearrange("k h t -> k (h t)"),
                     )
             return bank
@@ -339,7 +340,7 @@ def tile_transformerblock_pa_k_kernel(
             nc.vector.tensor_copy(out=sin_plus[:], in_=sin_bf16[:])
             nc.vector.tensor_scalar_mul(out=sin_minus[:], in0=sin_bf16[:], scalar1=-1.0)
 
-        def rotate(m, bank, heads, stores):
+        def rotate(m, bank, heads, stores, between=None):
             pairs = bank[:, 0 : 2 * PAIRS * heads].rearrange("p (h j e) -> p h j e", h=heads, e=2)
             other = rope_pool.tile([P, 2, HEADS, PAIRS], F32)
             nc.vector.tensor_tensor(
@@ -361,6 +362,8 @@ def tile_transformerblock_pa_k_kernel(
                 in1=cos_pair[:, m].unsqueeze(1).to_broadcast([P, heads, PAIRS, 2]),
                 op=ALU.mult,
             )
+            if between:
+                between()
             rotated = out_pool.tile([P, N_ROPE], F32)
             nc.vector.tensor_tensor(
                 out=rotated[:, 0 : 2 * PAIRS * heads].rearrange("p (n e) -> p n e", e=2),
@@ -384,8 +387,13 @@ def tile_transformerblock_pa_k_kernel(
         def finish(m, part):
             bank = acc_of[m, part]
             if m < TOKEN_TILES - 1:
-                keep_value(m, bank[:, N_ROPE:N_OUT], nc.vector.tensor_copy)
-                rotate(m, bank, HEADS, ((out_0, N_Q), (out_1, N_K)))
+                rotate(
+                    m,
+                    bank,
+                    HEADS,
+                    ((out_0, N_Q), (out_1, N_K)),
+                    lambda: keep_value(m, bank[:, N_ROPE:N_OUT], nc.vector.tensor_copy),
+                )
             elif part == 0:
                 rotate(m, bank, N_Q // (2 * PAIRS), ((out_0, N_Q),))
             else:

@@ -69,7 +69,7 @@ def tile_transformerblock_pa_k_kernel(
         code_pool = stack.enter_context(tc.tile_pool(name="code_pool", bufs=5))
         scrap_pool = stack.enter_context(tc.tile_pool(name="scrap_pool", bufs=1))
         small_pool = stack.enter_context(tc.tile_pool(name="small_pool", bufs=2))
-        out_pool = stack.enter_context(tc.tile_pool(name="out_pool", bufs=2))
+        out_pool = stack.enter_context(tc.tile_pool(name="out_pool", bufs=3))
         rope_pool = stack.enter_context(tc.tile_pool(name="rope_pool", bufs=1))
         bank_pool = stack.enter_context(tc.psum_pool(name="bank_pool", bufs=6))
         acc_pool = stack.enter_context(tc.psum_pool(name="acc_pool", bufs=2))
@@ -315,7 +315,10 @@ def tile_transformerblock_pa_k_kernel(
             k_pass = CHUNKS * (i % 2) + RUN * c + i // 2
             first, last = columns
             if (m, part) not in acc_of:
-                acc_of[m, part] = acc_pool.tile([P, N_OUT], F32, name="acc")
+                if part == 0:
+                    acc_of[m, part] = acc_pool.tile([P, N_OUT], F32, name="acc")
+                else:
+                    acc_of[m, part] = bank_pool.tile([P, N_OUT], F32, tag="bank", name="acc_late")
             ends = c == RUNS - 1 and i == 2 * RUN - 1
             nc.tensor.matmul_mx(
                 out=acc_of[m, part][:, 0 : last - first],
@@ -413,15 +416,15 @@ def tile_transformerblock_pa_k_kernel(
         for half in range(2):
             square_on_scalar(0, half)
             square_on_vector(1, half)
-        keep_gain(1, spreads[1], nc.vector.tensor_copy)
         for half in range(2):
             square_on_scalar(2, half)
             square_on_vector(3, half)
+        keep_gain(2, spreads[2], nc.scalar.copy)
+        keep_gain(3, spreads[3], nc.scalar.copy)
         rms = root(add_halves(add_squares(0)))
-        keep_gain(3, spreads[3], nc.vector.tensor_copy)
+        keep_gain(1, spreads[1], nc.vector.tensor_copy)
         keep_gain(4, spreads[4], nc.vector.tensor_copy)
         invert(0, rms)
-        keep_gain(2, spreads[2], nc.scalar.copy)
         for pair in range(6, 2 * RUNS):
             spreads.append(spread_gain(pair))
         for s in range(RUNS, SQUARES_AHEAD):
@@ -455,9 +458,10 @@ def tile_transformerblock_pa_k_kernel(
                 regroup(s - 1, transposed_of[s - 1], 1 if (squares_left and (s < 6 or not quantises and s % 2 == 1)) or s == ALL_RUNS else 0)
             if s == RUNS:
                 fill_rope_tables()
-            for m, part in to_rope:
-                finish(m, part)
-            to_rope.clear()
+            if s < ALL_RUNS - RUNS:
+                for m, part in to_rope:
+                    finish(m, part)
+                to_rope.clear()
             late = s - 1 if s > ALL_RUNS - RUNS else s - 2
             if late >= 0 and late // RUNS % 2 == 1:
                 quantise(late)

from contextlib import ExitStack

import concourse.mybir as mybir
from concourse.masks import make_identity

F32 = mybir.dt.float32
BF16 = mybir.dt.bfloat16
I32 = mybir.dt.int32
U32 = mybir.dt.uint32
U8 = mybir.dt.uint8
FP8X4 = mybir.dt.float8_e4m3fn_x4
ACT = mybir.ActivationFunctionType
ALU = mybir.AluOpType
AXIS = mybir.AxisListType

P = 128
TOKENS = 512
DIM = 16384
EPS = 1e-6
HALF = DIM // 2
GROUP = P // 2
GROUPS = TOKENS // GROUP
TOKEN_TILES = TOKENS // P
K_PASS = 4 * P
PASSES = DIM // K_PASS
RUN_K = 4 * K_PASS
RUN = RUN_K // K_PASS
BANK_K = 2 * K_PASS
RUNS = HALF // RUN_K
ALL_RUNS = GROUPS * RUNS
PLANE_COLUMNS = 16
CHUNKS = HALF // K_PASS
N_Q, N_K, N_V = 256, 128, 128
N_OUT = N_Q + N_K + N_V
N_ROPE = N_Q + N_K
HEADS = N_ROPE // 32
PAIRS = 16
SQUARES_AHEAD = RUNS + 1
PASSES_A_STEP = 7
WEIGHT_LAG = 5

FLOPS = 2 * TOKENS * DIM * N_OUT


def tile_transformerblock_pa_k_kernel(
    tc,
    x,
    freqs_cos,
    freqs_sin,
    wq_words,
    wq_scales,
    wk_words,
    wk_scales,
    wv_words,
    wv_scales,
    attn_norm_w,
    out_0,
    out_1,
    out_2,
):
    nc = tc.nc
    weights = ((wq_words, wq_scales, 0, N_Q), (wk_words, wk_scales, N_Q, N_K), (wv_words, wv_scales, N_ROPE, N_V))

    with ExitStack() as stack:
        keep = stack.enter_context(tc.tile_pool(name="keep", bufs=1))
        x_pool = stack.enter_context(tc.tile_pool(name="x_pool", bufs=12))
        h_pool = stack.enter_context(tc.tile_pool(name="h_pool", bufs=3))
        grouped_pool = stack.enter_context(tc.tile_pool(name="grouped_pool", bufs=RUNS + 1))
        code_pool = stack.enter_context(tc.tile_pool(name="code_pool", bufs=5))
        scrap_pool = stack.enter_context(tc.tile_pool(name="scrap_pool", bufs=1))
        small_pool = stack.enter_context(tc.tile_pool(name="small_pool", bufs=2))
        out_pool = stack.enter_context(tc.tile_pool(name="out_pool", bufs=3))
        rope_pool = stack.enter_context(tc.tile_pool(name="rope_pool", bufs=1))
        bank_pool = stack.enter_context(tc.psum_pool(name="bank_pool", bufs=6))
        acc_pool = stack.enter_context(tc.psum_pool(name="acc_pool", bufs=2))
        stack.enter_context(tc.manual_schedule())

        gain_rows = keep.tile([P, K_PASS], BF16)
        nc.vector.memset(gain_rows[:], 0.0)
        nc.sync.dma_start(out=gain_rows[0:PASSES, :], in_=attn_norm_w.rearrange("(c n) -> c n", n=K_PASS))

        x_halves = x.rearrange("t (h k) -> (t h) k", h=2)
        x_pieces = {}

        def load_x(s, half=None):
            g, c = divmod(s, RUNS)
            if s not in x_pieces:
                x_pieces[s] = x_pool.tile([P, RUN_K], BF16, name="piece")
            first, last = (0, RUN_K) if half is None else (BANK_K * half, BANK_K * (half + 1))
            nc.sync.dma_start(
                out=x_pieces[s][:, first:last], in_=x_halves[P * g : P * (g + 1), RUN_K * c + first : RUN_K * c + last]
            )

        for s in range(0, RUNS, 2):
            for half in range(2):
                for piece in (s, s + 1):
                    load_x(piece, half)
        for s in range(RUNS, 2 * RUNS):
            load_x(s)
        cos_bf16 = keep.tile([P, TOKEN_TILES, PAIRS], BF16)
        sin_bf16 = keep.tile([P, TOKEN_TILES, PAIRS], BF16)
        nc.sync.dma_start(out=cos_bf16[:], in_=freqs_cos.rearrange("(m p) j -> p m j", p=P))
        nc.sync.dma_start(out=sin_bf16[:], in_=freqs_sin.rearrange("(m p) j -> p m j", p=P))

        eps_col = keep.tile([P, 1], F32)
        nc.vector.memset(eps_col[:], EPS)
        warm = keep.tile([P, 1], F32)
        nc.scalar.activation(out=warm[:], in_=eps_col[:], func=ACT.Sqrt)

        sums = keep.tile([P, GROUPS, 2 * RUNS], F32)
        nc.vector.memset(sums[:], 0.0)
        rstd = keep.tile([P, GROUPS], F32)

        ident = keep.tile([P, P], F32)
        make_identity(nc, ident[:])

        select = keep.tile([P, CHUNKS, GROUP, 2], BF16)
        nc.vector.tensor_copy(
            out=select[:],
            in_=ident[:, 0:PASSES]
            .rearrange("k (h c) -> k c h", h=2)
            .unsqueeze(2)
            .to_broadcast([P, CHUNKS, GROUP, 2]),
        )
        by_half = ident[:].rearrange("k (t h) -> k h t", h=2)
        permute = keep.tile([P, 2, GROUP], F32)
        nc.vector.tensor_copy(out=permute[:], in_=by_half)
        both = keep.tile([P, GROUP, 2], F32)
        nc.vector.tensor_tensor(
            out=both[:],
            in0=by_half[:, 0].unsqueeze(2).to_broadcast([P, GROUP, 2]),
            in1=by_half[:, 1].unsqueeze(2).to_broadcast([P, GROUP, 2]),
            op=ALU.add,
        )
        w_planes = keep.tile([P, PLANE_COLUMNS, N_OUT], U8, align_bytes=64)
        nc.vector.memset(w_planes[:].rearrange("p a n -> p (a n)").bitcast(I32), 0)

        def load_scales(part):
            j, quadrant = divmod(part, 4)
            first_row = 32 * quadrant + 4 * j
            for unused_words, scales, first, width in weights:
                nc.sync.dma_start(
                    out=w_planes[first_row : first_row + 4, :, first : first + width].bitcast(I32),
                    in_=scales[PLANE_COLUMNS * j : PLANE_COLUMNS * (j + 1), 4 * quadrant : 4 * quadrant + 4, :]
                    .rearrange("a q n -> q a n")
                    .bitcast(I32),
                )

        w_words = keep.tile([P, PASSES, N_OUT], I32, align_bytes=64)

        def load_weights(block):
            c, h, part = block // 4, block // 2 % 2, block % 2
            passes = slice(CHUNKS * h + RUN * c, CHUNKS * h + RUN * (c + 1))
            for words, unused_scales, first, width in weights[:1] if part == 0 else weights[1:]:
                nc.sync.dma_start(
                    out=w_words[:, passes, first : first + width],
                    in_=words[passes].rearrange("g p n t -> p g (n t)").bitcast(I32),
                )

        load_x(2 * RUNS)
        load_scales(0)
        load_x(2 * RUNS + 1)
        load_scales(1)
        load_x(2 * RUNS + 2)
        load_scales(2)
        load_weights(0)
        load_scales(3)
        load_scales(4)
        load_weights(1)
        load_scales(5)
        load_x(2 * RUNS + 3)
        load_scales(6)
        load_weights(2)
        load_scales(7)

        gain = keep.tile([P, HALF], BF16)

        def spread_gain(pair):
            spread = bank_pool.tile([P, 2 * K_PASS], BF16, tag="bank")
            for half in range(2):
                c = 2 * pair + half
                nc.tensor.matmul(
                    out=spread[:, K_PASS * half : K_PASS * (half + 1)],
                    lhsT=select[:, c].rearrange("k t h -> k (t h)"),
                    rhs=gain_rows[:],
                    start=True,
                    stop=True,
                )
            return spread

        def keep_gain(pair, spread, copy_out):
            copy_out(out=gain[:, 2 * K_PASS * pair : 2 * K_PASS * (pair + 1)], in_=spread[:])

        def square_on_scalar(s, half=None):
            g, c = divmod(s, RUNS)
            columns = slice(0, RUN_K) if half is None else slice(BANK_K * half, BANK_K * (half + 1))
            place = c if half is None else c + half
            scrap = scrap_pool.tile([P, RUN_K], BF16)
            nc.scalar.activation(
                out=scrap[:, columns],
                in_=x_pieces[s][:, columns],
                func=ACT.Square,
                scale=1.0 / 128.0,
                accum_out=sums[:, g, place : place + 1],
            )

        def square_on_vector(s, half):
            g, c = divmod(s, RUNS)
            columns = slice(BANK_K * half, BANK_K * (half + 1))
            place = RUNS + c - 1 + half
            scrap = h_pool.tile([P, RUN_K], BF16, tag="h")
            nc.vector.scalar_tensor_tensor(
                out=scrap[:, columns],
                in0=x_pieces[s][:, columns],
                scalar=1.0 / DIM,
                in1=x_pieces[s][:, columns],
                op0=ALU.mult,
                op1=ALU.mult,
                accum_out=sums[:, g, place : place + 1],
            )

        def add_squares(g):
            half_sum = small_pool.tile([P, 1], F32)
            nc.vector.tensor_reduce(out=half_sum[:], in_=sums[:, g, :], axis=AXIS.X, op=ALU.add)
            return half_sum

        def add_halves(half_sum):
            mean_sq = bank_pool.tile([P, 1], F32, tag="bank")
            nc.tensor.matmul(
                out=mean_sq[:], lhsT=both[:].rearrange("k t h -> k (t h)"), rhs=half_sum[:], start=True, stop=True
            )
            return mean_sq

        def root(mean_sq):
            rms = small_pool.tile([P, 1], F32)
            nc.scalar.activation(out=rms[:], in_=mean_sq[:], func=ACT.Sqrt, bias=eps_col[:], scale=1.0)
            return rms

        def invert(g, rms):
            nc.vector.reciprocal(out=rstd[:, g : g + 1], in_=rms[:])

        def normalise(s):
            g, c = divmod(s, RUNS)
            h = h_pool.tile([P, 2, RUN_K // 4, 2], BF16, tag="h")
            x_words = x_pieces[s][:].rearrange("p (w u e) -> p u w e", u=2, e=2)
            gain_words = gain[:, RUN_K * c : RUN_K * (c + 1)].rearrange("p (w u e) -> p u w e", u=2, e=2)
            for u in range(2):
                nc.vector.scalar_tensor_tensor(
                    out=h[:, u],
                    in0=x_words[:, u],
                    scalar=rstd[:, g : g + 1],
                    in1=gain_words[:, u],
                    op0=ALU.mult,
                    op1=ALU.mult,
                )
            return h

        def transpose(h, b):
            h_words = h[:].rearrange("p u w e -> p (u w e)").bitcast(F32)
            bank = bank_pool.tile([P, 2, 2, P], F32, tag="bank")
            for u in range(2):
                for i in range(2):
                    first = P * (RUN * u + 2 * b + i)
                    nc.tensor.transpose(
                        out=bank[:, u, i, :],
                        in_=h_words[:, first : first + P],
                        identity=permute[:].rearrange("k h t -> k (h t)"),
                    )
            return bank

        grouped_tiles = {}

        def regroup(s, banks, vector_share):
            g, c = divmod(s, RUNS)
            m, part = divmod(g, 2)
            if (m, c) not in grouped_tiles:
                grouped_tiles[m, c] = grouped_pool.tile([P, 2 * RUN, P, 4], BF16, align_bytes=64, name="grouped")
            grouped_words = (
                grouped_tiles[m, c][:]
                .rearrange("p i j t -> p (i j t)")
                .bitcast(F32)
                .rearrange("p (i j u) -> p i j u", i=2 * RUN, u=2)
            )
            for b in range(RUN // 2):
                copy_out = nc.vector.tensor_copy if b >= RUN // 2 - vector_share else nc.scalar.copy
                copy_out(
                    out=grouped_words[:, 4 * b : 4 * b + 4, GROUP * part : GROUP * (part + 1)],
                    in_=banks[b][:].rearrange("p u i (h j) -> p (i h) j u", h=2),
                )

        waiting = []

        def quantise(s):
            g, c = divmod(s, RUNS)
            m = g // 2
            codes = code_pool.tile([P, 2 * RUN, P], U32, align_bytes=64)
            plane = code_pool.tile([P, 2 * RUN, P], U8, align_bytes=64)
            nc.vector.quantize_mx(
                out=codes[:].rearrange("p i j -> p (i j)").bitcast(FP8X4),
                scales=plane[:].rearrange("p i j -> p (i j)"),
                in_=grouped_tiles[m, c][:].rearrange("p i j t -> p (i j t)"),
            )
            parts = ((0, N_OUT),) if m < TOKEN_TILES - 1 else ((0, N_Q), (N_Q, N_OUT))
            earliest = 4 * (c if m == 0 else RUNS - 1) + WEIGHT_LAG
            for part in range(len(parts)):
                for i in range(2 * RUN):
                    waiting.append((earliest, s, part, parts[part], i, codes[:, i], plane[:, i]))

        acc_of = {}
        to_rope = []

        def project(s, part, columns, i, codes, plane):
            g, c = divmod(s, RUNS)
            m = g // 2
            k_pass = CHUNKS * (i % 2) + RUN * c + i // 2
            first, last = columns
            if (m, part) not in acc_of:
                if part == 0:
                    acc_of[m, part] = acc_pool.tile([P, N_OUT], F32, name="acc")
                else:
                    acc_of[m, part] = bank_pool.tile([P, N_OUT], F32, tag="bank", name="acc_late")
            ends = c == RUNS - 1 and i == 2 * RUN - 1
            nc.tensor.matmul_mx(
                out=acc_of[m, part][:, 0 : last - first],
                lhsT=codes.bitcast(FP8X4),
                lhsT_scale=plane,
                rhs=w_words[:, k_pass, first:last].bitcast(FP8X4),
                rhs_scale=w_planes[4 * (k_pass // PLANE_COLUMNS) : P, k_pass % PLANE_COLUMNS, first:last],
                start=c == 0 and i == 0,
                stop=ends,
            )
            if ends:
                to_rope.append((m, part))

        cos_pair = keep.tile([P, TOKEN_TILES, PAIRS, 2], F32)
        sin_plus = keep.tile([P, TOKEN_TILES, PAIRS], F32)
        sin_minus = keep.tile([P, TOKEN_TILES, PAIRS], F32)

        def fill_rope_tables():
            nc.vector.tensor_copy(
                out=cos_pair[:], in_=cos_bf16[:].unsqueeze(3).to_broadcast([P, TOKEN_TILES, PAIRS, 2])
            )
            nc.vector.tensor_copy(out=sin_plus[:], in_=sin_bf16[:])
            nc.vector.tensor_scalar_mul(out=sin_minus[:], in0=sin_bf16[:], scalar1=-1.0)

        def rotate(m, bank, heads, stores, between=None):
            pairs = bank[:, 0 : 2 * PAIRS * heads].rearrange("p (h j e) -> p h j e", h=heads, e=2)
            other = rope_pool.tile([P, 2, HEADS, PAIRS], F32)
            nc.vector.tensor_tensor(
                out=other[:, 0, 0:heads],
                in0=pairs[:, :, :, 1],
                in1=sin_minus[:, m].unsqueeze(1).to_broadcast([P, heads, PAIRS]),
                op=ALU.mult,
            )
            nc.vector.tensor_tensor(
                out=other[:, 1, 0:heads],
                in0=pairs[:, :, :, 0],
                in1=sin_plus[:, m].unsqueeze(1).to_broadcast([P, heads, PAIRS]),
                op=ALU.mult,
            )
            own = rope_pool.tile([P, HEADS, PAIRS, 2], F32)
            nc.vector.tensor_tensor(
                out=own[:, 0:heads],
                in0=pairs,
                in1=cos_pair[:, m].unsqueeze(1).to_broadcast([P, heads, PAIRS, 2]),
                op=ALU.mult,
            )
            if between:
                between()
            rotated = out_pool.tile([P, N_ROPE], F32)
            nc.vector.tensor_tensor(
                out=rotated[:, 0 : 2 * PAIRS * heads].rearrange("p (n e) -> p n e", e=2),
                in0=own[:, 0:heads].rearrange("p h j e -> p (h j) e"),
                in1=other[:, :, 0:heads].rearrange("p e h j -> p (h j) e"),
                op=ALU.add,
            )
            rows = slice(P * m, P * (m + 1))
            first = 0
            for out, width in stores:
                nc.sync.dma_start(
                    out=out[rows].rearrange("t h d -> t (h d)"), in_=rotated[:, first : first + width]
                )
                first += width

        def keep_value(m, columns, copy_out):
            value = out_pool.tile([P, N_V], F32)
            copy_out(out=value[:], in_=columns)
            nc.sync.dma_start(out=out_2[P * m : P * (m + 1)].rearrange("t h d -> t (h d)"), in_=value[:])

        def finish(m, part):
            bank = acc_of[m, part]
            if m < TOKEN_TILES - 1:
                rotate(
                    m,
                    bank,
                    HEADS,
                    ((out_0, N_Q), (out_1, N_K)),
                    lambda: keep_value(m, bank[:, N_ROPE:N_OUT], nc.vector.tensor_copy),
                )
            elif part == 0:
                rotate(m, bank, N_Q // (2 * PAIRS), ((out_0, N_Q),))
            else:
                rotate(m, bank, N_K // (2 * PAIRS), ((out_1, N_K),))
                keep_value(m, bank[:, N_K : N_K + N_V], nc.scalar.copy)

        def multiply(s, most):
            ready = [operands for operands in waiting[:most] if operands[0] <= s]
            for operands in ready:
                project(*operands[1:])
            waiting[:] = waiting[len(ready) :]

        spreads = []
        for pair in range(6):
            spreads.append(spread_gain(pair))
        keep_gain(0, spreads[0], nc.scalar.copy)
        for half in range(2):
            square_on_scalar(0, half)
            square_on_vector(1, half)
        for half in range(2):
            square_on_scalar(2, half)
            square_on_vector(3, half)
        keep_gain(2, spreads[2], nc.scalar.copy)
        keep_gain(3, spreads[3], nc.scalar.copy)
        rms = root(add_halves(add_squares(0)))
        keep_gain(1, spreads[1], nc.vector.tensor_copy)
        keep_gain(4, spreads[4], nc.vector.tensor_copy)
        invert(0, rms)
        for pair in range(6, 2 * RUNS):
            spreads.append(spread_gain(pair))
        for s in range(RUNS, SQUARES_AHEAD):
            square_on_scalar(s)

        transposed_of = {}
        for s in range(ALL_RUNS + 1):
            g, c = divmod(s, RUNS)
            squares_left = s + SQUARES_AHEAD < ALL_RUNS
            if c == 3 and g + 1 < GROUPS:
                mean_sq = add_halves(add_squares(g + 1))
                multiply(s, PASSES_A_STEP)
            if s < ALL_RUNS:
                h = normalise(s)
                if s + 3 * RUNS < ALL_RUNS:
                    load_x(s + 3 * RUNS)
                if s + 3 < 4 * RUNS:
                    load_weights(s + 3)
                if squares_left:
                    square_on_scalar(s + SQUARES_AHEAD)
                transposed_of[s] = [transpose(h, 0), transpose(h, 1)]
            if s == 0:
                keep_gain(5, spreads[5], nc.vector.tensor_copy)
            if s == 1:
                keep_gain(6, spreads[6], nc.vector.tensor_copy)
                keep_gain(7, spreads[7], nc.vector.tensor_copy)
            if c == 3 and g + 1 < GROUPS:
                rms = root(mean_sq)
            if s > 0:
                quantises = RUNS <= s - 2 and (s - 2) // RUNS % 2 == 1
                regroup(s - 1, transposed_of[s - 1], 1 if (squares_left and (s < 6 or not quantises and s % 2 == 1)) or s == ALL_RUNS else 0)
            if s == RUNS:
                fill_rope_tables()
            if s < ALL_RUNS - RUNS:
                for m, part in to_rope:
                    finish(m, part)
                to_rope.clear()
            late = s - 1 if s > ALL_RUNS - RUNS else s - 2
            if late >= 0 and late // RUNS % 2 == 1:
                quantise(late)
            if c != 2 or s > ALL_RUNS - 3:
                multiply(s, PASSES_A_STEP if s < ALL_RUNS - 3 else len(waiting))
            if c == 3 and g + 1 < GROUPS:
                invert(g + 1, rms)
        for m, part in to_rope:
            finish(m, part)
